import numpy as np
import ml_dtypes


def mxq(x, axis, fmt="e4m3"):
    dtype, down = {"e4m3": (ml_dtypes.float8_e4m3fn, 7), "e5m2": (ml_dtypes.float8_e5m2, 14)}[fmt]
    v = np.moveaxis(np.asarray(x, np.float32).astype(ml_dtypes.bfloat16).astype(np.float64), axis, -1)
    blocks = v.reshape(v.shape[:-1] + (-1, 32))
    amax = np.abs(blocks).max(-1, keepdims=True)
    byte = np.maximum(np.where(amax > 0, np.frexp(amax)[1] - 1 + 127, 0) - down, 1)
    scale = np.exp2(byte - 127.0)
    codes = (blocks / scale).astype(np.float32).astype(dtype).astype(np.float64)
    return np.moveaxis((codes * scale).reshape(v.shape), -1, axis)


WIDE = False


def mx_kscale(k):
    if not WIDE:
        return np.ones(k)
    levels = np.array([10, -10, 5, -5, 0])
    a = np.random.permutation(np.resize(levels, k // 512 * 4)).reshape(k // 512, 4)
    idx = np.arange(k)
    return np.exp2(a[idx // 512, idx % 128 // 32])


BF16 = ml_dtypes.bfloat16


def bf(x):
    return np.asarray(x, np.float32).astype(BF16)


def f64(x):
    return np.asarray(x).astype(np.float64)


NU, NI, NE, EMB = 384, 640, 1024, 512
N = NU + NI
LN_EPS = 1e-5
DENS = 0.01
A_SCALE = (1.5e-4 / ((NE * DENS) ** 2 + N * NE * DENS ** 2 * (1.0 + NE * DENS ** 2))) ** 0.25


def setup_inputs():
    s = mx_kscale(N)
    adj = (np.random.uniform(size=(N, NE)) < DENS) * np.random.uniform(0.5, 1.5, (N, NE)) * A_SCALE
    return {"e_nodes": bf(np.random.standard_normal((N, EMB)) / s[:, None]),
            "adj": bf(adj * s[:, None]),
            "ego_embeddings": bf(np.random.standard_normal((N, EMB))),
            "ln_gamma": bf(1.0 + 0.1 * np.random.standard_normal(EMB)),
            "ln_beta": bf(0.1 * np.random.standard_normal(EMB))}


def reference(e_nodes, adj, ego_embeddings, ln_gamma, ln_beta):
    a = f64(adj)
    m = mxq(a.T, 1, "e4m3") @ mxq(f64(e_nodes), 0, "e4m3")
    h = mxq(a, 1, "e4m3") @ mxq(m, 0, "e4m3")
    mu = h.mean(-1, keepdims=True)
    var = h.var(-1, keepdims=True)
    return (h - mu) * (1.0 / np.sqrt(var + LN_EPS)) * f64(ln_gamma) + f64(ln_beta) + f64(ego_embeddings)

@@ -1,0 +1,235 @@
+from contextlib import ExitStack
+
+import concourse.mybir as mybir
+from concourse.masks import make_identity
+
+F32 = mybir.dt.float32
+BF16 = mybir.dt.bfloat16
+U32 = mybir.dt.uint32
+U8 = mybir.dt.uint8
+FP8X4 = mybir.dt.float8_e4m3fn_x4
+ALU = mybir.AluOpType
+ACT = mybir.ActivationFunctionType
+
+P = 128
+EMB = 512
+LN_EPS = 1e-5
+FLOPS = 2 * 2 * 1024 * 1024 * 512
+
+MANUAL = True
+A_ON_SCALAR = ((0, 1), (1, 0))
+
+
+def tile_hgnnmodel_pa_kernel(tc, e_nodes, adj, ego_embeddings, ln_gamma, ln_beta, out):
+    nc = tc.nc
+    with ExitStack() as ctx:
+        keep = ctx.enter_context(tc.tile_pool(name="keep", bufs=1))
+        work = ctx.enter_context(tc.tile_pool(name="work", bufs=3))
+        small = ctx.enter_context(tc.tile_pool(name="small", bufs=4))
+        psum = ctx.enter_context(tc.psum_pool(name="psum", bufs=1))
+        if MANUAL:
+            ctx.enter_context(tc.manual_schedule())
+
+        def bank(b, shape, name):
+            return psum.tile(shape, F32, tag="bank%d" % b, name=name)
+
+        gb_rows = keep.tile([P, 2 * EMB], BF16, name="gb_rows")
+        nc.vector.memset(gb_rows[:], 0.0)
+        ones = keep.tile([P, P], BF16, name="ones")
+        nc.vector.memset(ones[:], 1.0)
+        one_col = keep.tile([P, 1], F32, name="one_col")
+        nc.vector.memset(one_col[:], 1.0)
+        nc.scalar.dma_start(out=gb_rows[0:1, 0:EMB], in_=ln_gamma.unsqueeze(0))
+        nc.scalar.dma_start(out=gb_rows[0:1, EMB : 2 * EMB], in_=ln_beta.unsqueeze(0))
+        ident = keep.tile([P, P], F32, name="ident")
+        make_identity(nc, ident[:])
+        eps_t = keep.tile([P, 1], F32, name="eps_t")
+        nc.scalar.mul(out=eps_t[:], in_=one_col[:], mul=LN_EPS)
+
+        e_raw = [keep.tile([P, 4, EMB], BF16, name="e_raw%d" % c) for c in range(2)]
+        a_raw = [[keep.tile([P, 4, 512], BF16, name="a_raw%d%d" % (g, c)) for c in range(2)] for g in range(2)]
+        ego_raw = [keep.tile([P, 4, EMB], BF16, name="ego_raw%d" % c) for c in range(2)]
+
+        def load_e(c):
+            nc.sync.dma_start(
+                out=e_raw[c][:], in_=e_nodes[512 * c : 512 * (c + 1), :].rearrange("(p j) f -> p j f", j=4)
+            )
+
+        def load_a(g, c):
+            nc.sync.dma_start(
+                out=a_raw[g][c][:],
+                in_=adj[512 * c : 512 * (c + 1), 512 * g : 512 * (g + 1)].rearrange("(p j) e -> p j e", j=4),
+            )
+
+        load_a(0, 0)
+        load_e(0)
+        load_a(0, 1)
+        load_e(1)
+        load_a(1, 0)
+        load_a(1, 1)
+        for c in range(2):
+            nc.sync.dma_start(
+                out=ego_raw[c][:], in_=ego_embeddings[512 * c : 512 * (c + 1), :].rearrange("(p j) f -> p j f", j=4)
+            )
+
+        gamma_b = keep.tile([P, EMB], F32, name="gamma_b")
+        beta_b = keep.tile([P, EMB], F32, name="beta_b")
+        for i, dst in enumerate((gamma_b, beta_b)):
+            bc = bank(6 + i, [P, EMB], "bc%d" % i)
+            nc.tensor.matmul(out=bc[:], lhsT=ones[:], rhs=gb_rows[:, EMB * i : EMB * (i + 1)], start=True, stop=True)
+            nc.scalar.copy(out=dst[:], in_=bc[:])
+
+        ge = [keep.tile([P, EMB, 4], BF16, name="ge%d" % c, align_bytes=64) for c in range(2)]
+        e_codes = [keep.tile([P, EMB], U32, name="ec%d" % c, align_bytes=64) for c in range(2)]
+        e_scales = [keep.tile([P, EMB], U8, name="es%d" % c, align_bytes=64) for c in range(2)]
+        ga = [[keep.tile([P, 512, 4], BF16, name="ga%d%d" % (g, c), align_bytes=64) for c in range(2)] for g in range(2)]
+        a1_codes = [[keep.tile([P, 512], U32, name="a1c%d%d" % (g, c), align_bytes=64) for c in range(2)] for g in range(2)]
+        a1_scales = [[keep.tile([P, 512], U8, name="a1s%d%d" % (g, c), align_bytes=64) for c in range(2)] for g in range(2)]
+        gb = [[keep.tile([P, 4, P, 2], F32, name="gb%d%d" % (g, c), align_bytes=64) for c in range(2)] for g in range(2)]
+        a2_codes = [[keep.tile([P, 512], U32, name="a2c%d%d" % (g, c), align_bytes=64) for c in range(2)] for g in range(2)]
+        a2_scales = [[keep.tile([P, 512], U8, name="a2s%d%d" % (g, c), align_bytes=64) for c in range(2)] for g in range(2)]
+        gm = [keep.tile([P, EMB, 4], BF16, name="gm%d" % g, align_bytes=64) for g in range(2)]
+        m_codes = [keep.tile([P, EMB], U32, name="mc%d" % g, align_bytes=64) for g in range(2)]
+        m_scales = [keep.tile([P, EMB], U8, name="ms%d" % g, align_bytes=64) for g in range(2)]
+
+        def regroup_e(c):
+            nc.vector.tensor_copy(
+                out=ge[c][:].rearrange("p (a i) t -> p a t i", i=4),
+                in_=e_raw[c][:].rearrange("p t (a i) -> p a t i", i=4),
+            )
+
+        def quantise_e(c):
+            nc.vector.quantize_mx(
+                out=e_codes[c][:].bitcast(FP8X4), scales=e_scales[c][:], in_=ge[c][:].rearrange("p w j -> p (w j)")
+            )
+
+        def regroup_a(g, c):
+            for u in range(2):
+                src = a_raw[g][c][:, :, 256 * u : 256 * (u + 1)].rearrange("p j (q s) -> p s q j", s=2)
+                dst = ga[g][c][:, 256 * u : 256 * (u + 1), :].rearrange("p (s q) j -> p s q j", s=2)
+                if u == 1 and (g, c) in A_ON_SCALAR:
+                    nc.scalar.copy(out=dst, in_=src)
+                else:
+                    nc.vector.tensor_copy(out=dst, in_=src)
+
+        def quantise_a1(g, c):
+            nc.vector.quantize_mx(
+                out=a1_codes[g][c][:].bitcast(FP8X4),
+                scales=a1_scales[g][c][:],
+                in_=ga[g][c][:].rearrange("p w j -> p (w j)"),
+            )
+
+        def transpose_a(g, c):
+            a32 = a_raw[g][c][:].bitcast(F32)
+            banks = []
+            for jp in range(2):
+                xt = bank(4 * g + 2 * c + jp, [P, 4, P], "xt%d%d%d" % (g, c, jp))
+                for jj in range(2):
+                    for u in range(2):
+                        nc.tensor.transpose(xt[:, 2 * jj + u, :], a32[:, 2 * jp + jj, P * u : P * (u + 1)], ident[:])
+                banks.append(xt)
+            return banks
+
+        def copy_xt(g, c, banks):
+            for jp in range(2):
+                nc.scalar.copy(
+                    out=gb[g][c][:, 2 * jp : 2 * jp + 2, :, :],
+                    in_=banks[jp][:].rearrange("q (jj u) n -> q jj n u", u=2),
+                )
+
+        def quantise_a2(g, c):
+            nc.vector.quantize_mx(
+                out=a2_codes[g][c][:].bitcast(FP8X4),
+                scales=a2_scales[g][c][:],
+                in_=gb[g][c][:].bitcast(BF16).rearrange("q j n w -> q (j n w)"),
+            )
+
+        items = (("a", 0, 0), ("e", 0, 0), ("a", 0, 1), ("e", 1, 1), ("a", 1, 0), ("a", 1, 1))
+
+        def quantise_item(item):
+            if item[0] == "e":
+                quantise_e(item[1])
+            else:
+                quantise_a1(item[1], item[2])
+
+        for i, item in enumerate(items):
+            if item[0] == "e":
+                regroup_e(item[1])
+            else:
+                banks = transpose_a(item[1], item[2])
+                regroup_a(item[1], item[2])
+                copy_xt(item[1], item[2], banks)
+            if i > 0:
+                quantise_item(items[i - 1])
+        quantise_item(items[-1])
+
+        ebs = []
+        for nt in range(8):
+            c, j = divmod(nt, 4)
+            eb = keep.tile([P, EMB], F32, name="eb%d" % nt)
+            nc.gpsimd.tensor_tensor(out=eb[:], in0=ego_raw[c][:, j, :], in1=beta_b[:], op=ALU.add)
+            ebs.append(eb)
+
+        def quantise_m(g, half):
+            cols = slice(256 * half, 256 * (half + 1))
+            nc.vector.quantize_mx(
+                out=m_codes[g][:, cols].bitcast(FP8X4),
+                scales=m_scales[g][:, cols],
+                in_=gm[g][:, cols, :].rearrange("p w j -> p (w j)"),
+            )
+
+        for g in range(2):
+            quantise_a2(g, 0)
+            for fc in range(4):
+                mp = bank(4 * g + fc, [P, 4, P], "mp%d%d" % (g, fc))
+                for t in range(4):
+                    for c in range(2):
+                        nc.tensor.matmul_mx(
+                            out=mp[:, t, :],
+                            lhsT=a1_codes[g][c][:, P * t : P * (t + 1)].bitcast(FP8X4),
+                            lhsT_scale=a1_scales[g][c][:, P * t : P * (t + 1)],
+                            rhs=e_codes[c][:, P * fc : P * (fc + 1)].bitcast(FP8X4),
+                            rhs_scale=e_scales[c][:, P * fc : P * (fc + 1)],
+                            start=(c == 0),
+                            stop=(c == 1),
+                        )
+                nc.scalar.copy(out=gm[g][:, P * fc : P * (fc + 1), :], in_=mp[:].rearrange("p t f -> p f t"))
+                if fc == 1:
+                    quantise_a2(g, 1)
+                    quantise_m(g, 0)
+            quantise_m(g, 1)
+
+        out_v = out.rearrange("(c p j) f -> p c j f", c=2, j=4)
+        junk = keep.tile([P, EMB], BF16, name="junk")
+        for nt in range(8):
+            c, j = divmod(nt, 4)
+            hp = bank(nt, [P, EMB], "hp%d" % nt)
+            for g in range(2):
+                nc.tensor.matmul_mx(
+                    out=hp[:],
+                    lhsT=a2_codes[g][c][:, P * j : P * (j + 1)].bitcast(FP8X4),
+                    lhsT_scale=a2_scales[g][c][:, P * j : P * (j + 1)],
+                    rhs=m_codes[g][:].bitcast(FP8X4),
+                    rhs_scale=m_scales[g][:],
+                    start=(g == 0),
+                    stop=(g == 1),
+                )
+            hsum = small.tile([P, 1], F32, name="hsum")
+            negmean = small.tile([P, 1], F32, name="negmean")
+            ssd = small.tile([P, 1], F32, name="ssd")
+            std = small.tile([P, 1], F32, name="std")
+            rstd = small.tile([P, 1], F32, name="rstd")
+            nc.scalar.activation(out=junk[:], in_=hp[:], func=ACT.Identity, accum_out=hsum[:])
+            nc.scalar.mul(out=negmean[:], in_=hsum[:], mul=-1.0 / EMB)
+            nc.scalar.activation(out=junk[:], in_=hp[:], func=ACT.Square, bias=negmean[:], accum_out=ssd[:])
+            nc.scalar.activation(out=std[:], in_=ssd[:], func=ACT.Sqrt, bias=eps_t[:], scale=1.0 / EMB)
+            u_ = work.tile([P, EMB], F32, name="u_")
+            nc.vector.scalar_tensor_tensor(
+                out=u_[:], in0=hp[:], scalar=negmean[:], in1=gamma_b[:], op0=ALU.add, op1=ALU.mult
+            )
+            nc.vector.reciprocal(out=rstd[:], in_=std[:])
+            o_ = work.tile([P, EMB], F32, name="o_", bufs=4)
+            nc.vector.scalar_tensor_tensor(
+                out=o_[:], in0=u_[:], scalar=rstd[:], in1=ebs[nt][:], op0=ALU.mult, op1=ALU.add
+            )
+            nc.sync.dma_start(out=out_v[:, c, j, :], in_=o_[:])

@@ -18,6 +18,7 @@ FLOPS = 2 * 2 * 1024 * 1024 * 512
 
 MANUAL = True
 A_ON_SCALAR = ((0, 1), (1, 0))
+STATS_ON_VECTOR = (0, 2)
 
 
 def tile_hgnnmodel_pa_kernel(tc, e_nodes, adj, ego_embeddings, ln_gamma, ln_beta, out):
@@ -39,8 +40,6 @@ def tile_hgnnmodel_pa_kernel(tc, e_nodes, adj, ego_embeddings, ln_gamma, ln_beta
         nc.vector.memset(ones[:], 1.0)
         one_col = keep.tile([P, 1], F32, name="one_col")
         nc.vector.memset(one_col[:], 1.0)
-        nc.scalar.dma_start(out=gb_rows[0:1, 0:EMB], in_=ln_gamma.unsqueeze(0))
-        nc.scalar.dma_start(out=gb_rows[0:1, EMB : 2 * EMB], in_=ln_beta.unsqueeze(0))
         ident = keep.tile([P, P], F32, name="ident")
         make_identity(nc, ident[:])
         eps_t = keep.tile([P, 1], F32, name="eps_t")
@@ -63,6 +62,8 @@ def tile_hgnnmodel_pa_kernel(tc, e_nodes, adj, ego_embeddings, ln_gamma, ln_beta
 
         load_a(0, 0)
         load_e(0)
+        nc.sync.dma_start(out=gb_rows[0:1, 0:EMB], in_=ln_gamma.unsqueeze(0))
+        nc.sync.dma_start(out=gb_rows[0:1, EMB : 2 * EMB], in_=ln_beta.unsqueeze(0))
         load_a(0, 1)
         load_e(1)
         load_a(1, 0)
@@ -74,10 +75,14 @@ def tile_hgnnmodel_pa_kernel(tc, e_nodes, adj, ego_embeddings, ln_gamma, ln_beta
 
         gamma_b = keep.tile([P, EMB], F32, name="gamma_b")
         beta_b = keep.tile([P, EMB], F32, name="beta_b")
-        for i, dst in enumerate((gamma_b, beta_b)):
-            bc = bank(6 + i, [P, EMB], "bc%d" % i)
-            nc.tensor.matmul(out=bc[:], lhsT=ones[:], rhs=gb_rows[:, EMB * i : EMB * (i + 1)], start=True, stop=True)
-            nc.scalar.copy(out=dst[:], in_=bc[:])
+
+        def spread_gamma_beta():
+            for i, dst in enumerate((gamma_b, beta_b)):
+                bc = bank(i, [P, EMB], "bc%d" % i)
+                nc.tensor.matmul(
+                    out=bc[:], lhsT=ones[:], rhs=gb_rows[:, EMB * i : EMB * (i + 1)], start=True, stop=True
+                )
+                nc.scalar.copy(out=dst[:], in_=bc[:])
 
         ge = [keep.tile([P, EMB, 4], BF16, name="ge%d" % c, align_bytes=64) for c in range(2)]
         e_codes = [keep.tile([P, EMB], U32, name="ec%d" % c, align_bytes=64) for c in range(2)]
@@ -161,6 +166,8 @@ def tile_hgnnmodel_pa_kernel(tc, e_nodes, adj, ego_embeddings, ln_gamma, ln_beta
                 copy_xt(item[1], item[2], banks)
             if i > 0:
                 quantise_item(items[i - 1])
+            if i == 4:
+                spread_gamma_beta()
         quantise_item(items[-1])
 
         ebs = []
@@ -199,37 +206,88 @@ def tile_hgnnmodel_pa_kernel(tc, e_nodes, adj, ego_embeddings, ln_gamma, ln_beta
                     quantise_m(g, 0)
             quantise_m(g, 1)
 
+        hps = [bank(nt, [P, EMB], "hp%d" % nt) for nt in range(8)]
+
+        def second_matmul(nt, g):
+            c, j = divmod(nt, 4)
+            nc.tensor.matmul_mx(
+                out=hps[nt][:],
+                lhsT=a2_codes[g][c][:, P * j : P * (j + 1)].bitcast(FP8X4),
+                lhsT_scale=a2_scales[g][c][:, P * j : P * (j + 1)],
+                rhs=m_codes[g][:].bitcast(FP8X4),
+                rhs_scale=m_scales[g][:],
+                start=(g == 0),
+                stop=(g == 1),
+            )
+
+        for half in range(2):
+            for g in range(2):
+                for nt in range(4 * half, 4 * half + 4):
+                    second_matmul(nt, g)
+
         out_v = out.rearrange("(c p j) f -> p c j f", c=2, j=4)
         junk = keep.tile([P, EMB], BF16, name="junk")
+
+        def on_scalar(nt):
+            return 0 <= nt < 8 and nt not in STATS_ON_VECTOR
+
+        hsum = {}
+        shift = {}
+        ssd = {}
+        mv = {}
         for nt in range(8):
-            c, j = divmod(nt, 4)
-            hp = bank(nt, [P, EMB], "hp%d" % nt)
-            for g in range(2):
-                nc.tensor.matmul_mx(
-                    out=hp[:],
-                    lhsT=a2_codes[g][c][:, P * j : P * (j + 1)].bitcast(FP8X4),
-                    lhsT_scale=a2_scales[g][c][:, P * j : P * (j + 1)],
-                    rhs=m_codes[g][:].bitcast(FP8X4),
-                    rhs_scale=m_scales[g][:],
-                    start=(g == 0),
-                    stop=(g == 1),
+            if on_scalar(nt):
+                hsum[nt] = keep.tile([P, 1], F32, name="hsum%d" % nt)
+                shift[nt] = keep.tile([P, 1], F32, name="shift%d" % nt)
+                ssd[nt] = keep.tile([P, 1], F32, name="ssd%d" % nt)
+            else:
+                mv[nt] = keep.tile([P, 2], F32, name="mv%d" % nt)
+        std = [keep.tile([P, 1], F32, name="std%d" % nt) for nt in range(8)]
+        rstd = [keep.tile([P, 1], F32, name="rstd%d" % nt) for nt in range(8)]
+        us = [keep.tile([P, EMB], F32, name="u%d" % nt) for nt in range(8)]
+
+        def row_sums(nt):
+            if on_scalar(nt):
+                nc.scalar.activation(out=junk[:], in_=hps[nt][:], func=ACT.Identity, accum_out=hsum[nt][:])
+
+        for nt in STATS_ON_VECTOR:
+            st6 = small.tile([P, 6], F32, name="st6")
+            nc.vector.bn_stats(out=st6[:], in_=hps[nt][:])
+            nc.vector.bn_aggr(out=mv[nt][:], in_=st6[:])
+        row_sums(0)
+        for k in range(9):
+            if on_scalar(k):
+                nc.scalar.mul(out=shift[k][:], in_=hsum[k][:], mul=-1.0 / EMB)
+            row_sums(k + 1)
+            if k >= 1:
+                if on_scalar(k - 1):
+                    nc.scalar.activation(
+                        out=std[k - 1][:], in_=ssd[k - 1][:], func=ACT.Sqrt, bias=eps_t[:], scale=1.0 / EMB
+                    )
+                else:
+                    nc.scalar.activation(
+                        out=std[k - 1][:], in_=mv[k - 1][:, 1:2], func=ACT.Sqrt, bias=eps_t[:], scale=1.0
+                    )
+            if on_scalar(k):
+                nc.scalar.activation(
+                    out=junk[:], in_=hps[k][:], func=ACT.Square, bias=shift[k][:], accum_out=ssd[k][:]
                 )
-            hsum = small.tile([P, 1], F32, name="hsum")
-            negmean = small.tile([P, 1], F32, name="negmean")
-            ssd = small.tile([P, 1], F32, name="ssd")
-            std = small.tile([P, 1], F32, name="std")
-            rstd = small.tile([P, 1], F32, name="rstd")
-            nc.scalar.activation(out=junk[:], in_=hp[:], func=ACT.Identity, accum_out=hsum[:])
-            nc.scalar.mul(out=negmean[:], in_=hsum[:], mul=-1.0 / EMB)
-            nc.scalar.activation(out=junk[:], in_=hp[:], func=ACT.Square, bias=negmean[:], accum_out=ssd[:])
-            nc.scalar.activation(out=std[:], in_=ssd[:], func=ACT.Sqrt, bias=eps_t[:], scale=1.0 / EMB)
-            u_ = work.tile([P, EMB], F32, name="u_")
-            nc.vector.scalar_tensor_tensor(
-                out=u_[:], in0=hp[:], scalar=negmean[:], in1=gamma_b[:], op0=ALU.add, op1=ALU.mult
-            )
-            nc.vector.reciprocal(out=rstd[:], in_=std[:])
-            o_ = work.tile([P, EMB], F32, name="o_", bufs=4)
-            nc.vector.scalar_tensor_tensor(
-                out=o_[:], in0=u_[:], scalar=rstd[:], in1=ebs[nt][:], op0=ALU.mult, op1=ALU.add
-            )
-            nc.sync.dma_start(out=out_v[:, c, j, :], in_=o_[:])
+            if k >= 1:
+                nc.vector.reciprocal(out=rstd[k - 1][:], in_=std[k - 1][:])
+            if k < 8:
+                if on_scalar(k):
+                    nc.vector.scalar_tensor_tensor(
+                        out=us[k][:], in0=hps[k][:], scalar=shift[k][:], in1=gamma_b[:], op0=ALU.add, op1=ALU.mult
+                    )
+                else:
+                    nc.vector.scalar_tensor_tensor(
+                        out=us[k][:], in0=hps[k][:], scalar=mv[k][:, 0:1], in1=gamma_b[:],
+                        op0=ALU.subtract, op1=ALU.mult,
+                    )
+            if k >= 1:
+                c, j = divmod(k - 1, 4)
+                o_ = work.tile([P, EMB], F32, name="o_", bufs=4)
+                nc.vector.scalar_tensor_tensor(
+                    out=o_[:], in0=us[k - 1][:], scalar=rstd[k - 1][:], in1=ebs[k - 1][:], op0=ALU.mult, op1=ALU.add
+                )
+                nc.sync.dma_start(out=out_v[:, c, j, :], in_=o_[:])

@@ -19,6 +19,7 @@ FLOPS = 2 * 2 * 1024 * 1024 * 512
 MANUAL = True
 A_ON_SCALAR = ((0, 1), (1, 0))
 STATS_ON_VECTOR = (0, 2)
+EB_ON_VECTOR = 3
 
 
 def tile_hgnnmodel_pa_kernel(tc, e_nodes, adj, ego_embeddings, ln_gamma, ln_beta, out):
@@ -42,6 +43,8 @@ def tile_hgnnmodel_pa_kernel(tc, e_nodes, adj, ego_embeddings, ln_gamma, ln_beta
         nc.vector.memset(one_col[:], 1.0)
         ident = keep.tile([P, P], F32, name="ident")
         make_identity(nc, ident[:])
+        ident_bf = keep.tile([P, P], BF16, name="ident_bf")
+        make_identity(nc, ident_bf[:])
         eps_t = keep.tile([P, 1], F32, name="eps_t")
         nc.scalar.mul(out=eps_t[:], in_=one_col[:], mul=LN_EPS)
 
@@ -170,12 +173,18 @@ def tile_hgnnmodel_pa_kernel(tc, e_nodes, adj, ego_embeddings, ln_gamma, ln_beta
                 spread_gamma_beta()
         quantise_item(items[-1])
 
-        ebs = []
-        for nt in range(8):
+        ebs = {}
+
+        def add_beta_on_vector(nt):
             c, j = divmod(nt, 4)
-            eb = keep.tile([P, EMB], F32, name="eb%d" % nt)
-            nc.gpsimd.tensor_tensor(out=eb[:], in0=ego_raw[c][:, j, :], in1=beta_b[:], op=ALU.add)
-            ebs.append(eb)
+            ebs[nt] = keep.tile([P, EMB], F32, name="eb%d" % nt)
+            nc.vector.tensor_tensor(out=ebs[nt][:], in0=ego_raw[c][:, j, :], in1=beta_b[:], op=ALU.add)
+
+        def add_beta_on_tensor(nt):
+            c, j = divmod(nt, 4)
+            ebs[nt] = bank(nt - EB_ON_VECTOR, [P, EMB], "ebp%d" % nt)
+            nc.tensor.matmul(out=ebs[nt][:], lhsT=ident_bf[:], rhs=ego_raw[c][:, j, :], start=True, stop=False)
+            nc.tensor.matmul(out=ebs[nt][:], lhsT=ones[:], rhs=gb_rows[:, EMB : 2 * EMB], start=False, stop=True)
 
         def quantise_m(g, half):
             cols = slice(256 * half, 256 * (half + 1))
@@ -204,7 +213,9 @@ def tile_hgnnmodel_pa_kernel(tc, e_nodes, adj, ego_embeddings, ln_gamma, ln_beta
                 if fc == 1:
                     quantise_a2(g, 1)
                     quantise_m(g, 0)
+                    add_beta_on_vector(g)
             quantise_m(g, 1)
+        add_beta_on_vector(2)
 
         hps = [bank(nt, [P, EMB], "hp%d" % nt) for nt in range(8)]
 
@@ -284,6 +295,8 @@ def tile_hgnnmodel_pa_kernel(tc, e_nodes, adj, ego_embeddings, ln_gamma, ln_beta
                         out=us[k][:], in0=hps[k][:], scalar=mv[k][:, 0:1], in1=gamma_b[:],
                         op0=ALU.subtract, op1=ALU.mult,
                     )
+            if EB_ON_VECTOR <= k + EB_ON_VECTOR < 8:
+                add_beta_on_tensor(k + EB_ON_VECTOR)
             if k >= 1:
                 c, j = divmod(k - 1, 4)
                 o_ = work.tile([P, EMB], F32, name="o_", bufs=4)

@@ -45,6 +45,8 @@ def tile_hgnnmodel_pa_kernel(tc, e_nodes, adj, ego_embeddings, ln_gamma, ln_beta
         make_identity(nc, ident[:])
         ident_bf = keep.tile([P, P], BF16, name="ident_bf")
         make_identity(nc, ident_bf[:])
+        warm = keep.tile([P, 1], F32, name="warm")
+        nc.scalar.activation(out=warm[:], in_=one_col[:], func=ACT.Sqrt)
         eps_t = keep.tile([P, 1], F32, name="eps_t")
         nc.scalar.mul(out=eps_t[:], in_=one_col[:], mul=LN_EPS)
 

@@ -5,6 +5,7 @@ from concourse.masks import make_identity
 
 F32 = mybir.dt.float32
 BF16 = mybir.dt.bfloat16
+I32 = mybir.dt.int32
 U32 = mybir.dt.uint32
 U8 = mybir.dt.uint8
 FP8X4 = mybir.dt.float8_e4m3fn_x4
@@ -16,27 +17,56 @@ EMB = 512
 LN_EPS = 1e-5
 FLOPS = 2 * 2 * 1024 * 1024 * 512
 
-MANUAL = True
 A_ON_SCALAR = ((0, 1), (1, 0))
 STATS_ON_VECTOR = (0, 2)
-EB_ON_VECTOR = 3
+EB_ON_GPSIMD = 3
+A_FORM = "write contiguous"
 
 
 def tile_hgnnmodel_pa_kernel(tc, e_nodes, adj, ego_embeddings, ln_gamma, ln_beta, out):
     nc = tc.nc
     with ExitStack() as ctx:
         keep = ctx.enter_context(tc.tile_pool(name="keep", bufs=1))
-        work = ctx.enter_context(tc.tile_pool(name="work", bufs=3))
-        small = ctx.enter_context(tc.tile_pool(name="small", bufs=4))
+        work = ctx.enter_context(tc.tile_pool(name="work", bufs=4))
         psum = ctx.enter_context(tc.psum_pool(name="psum", bufs=1))
-        if MANUAL:
-            ctx.enter_context(tc.manual_schedule())
+        ctx.enter_context(tc.manual_schedule())
 
         def bank(b, shape, name):
             return psum.tile(shape, F32, tag="bank%d" % b, name=name)
 
+        def grid(shape, dtype, name):
+            return [
+                [keep.tile(shape, dtype, name="%s%d%d" % (name, g, c), align_bytes=64) for c in range(2)]
+                for g in range(2)
+            ]
+
+        def pair(shape, dtype, name):
+            return [keep.tile(shape, dtype, name="%s%d" % (name, i), align_bytes=64) for i in range(2)]
+
+        rows_in = keep.tile([1, 2 * EMB], BF16, name="rows_in")
+        e_raw = pair([P, 4, EMB], BF16, "e_raw")
+        a_raw = grid([P, 4, 512], BF16, "a_raw")
+        ego_raw = pair([P, 4, EMB], BF16, "ego_raw")
+
+        def load_rows(dst, src, c):
+            nc.sync.dma_start(out=dst[:], in_=src[512 * c : 512 * (c + 1), :].rearrange("(p j) f -> p j f", j=4))
+
+        def load_a(g, c):
+            load_rows(a_raw[g][c], adj[:, 512 * g : 512 * (g + 1)], c)
+
+        nc.sync.dma_start(out=rows_in[:, 0:EMB], in_=ln_gamma.unsqueeze(0))
+        nc.sync.dma_start(out=rows_in[:, EMB : 2 * EMB], in_=ln_beta.unsqueeze(0))
+        load_a(0, 0)
+        load_rows(e_raw[0], e_nodes, 0)
+        load_a(0, 1)
+        load_rows(e_raw[1], e_nodes, 1)
+        load_a(1, 0)
+        load_a(1, 1)
+        load_rows(ego_raw[0], ego_embeddings, 0)
+        load_rows(ego_raw[1], ego_embeddings, 1)
+
         gb_rows = keep.tile([P, 2 * EMB], BF16, name="gb_rows")
-        nc.vector.memset(gb_rows[:], 0.0)
+        nc.vector.memset(gb_rows[:].bitcast(I32), 0)
         ones = keep.tile([P, P], BF16, name="ones")
         nc.vector.memset(ones[:], 1.0)
         one_col = keep.tile([P, 1], F32, name="one_col")
@@ -50,57 +80,26 @@ def tile_hgnnmodel_pa_kernel(tc, e_nodes, adj, ego_embeddings, ln_gamma, ln_beta
         eps_t = keep.tile([P, 1], F32, name="eps_t")
         nc.scalar.mul(out=eps_t[:], in_=one_col[:], mul=LN_EPS)
 
-        e_raw = [keep.tile([P, 4, EMB], BF16, name="e_raw%d" % c) for c in range(2)]
-        a_raw = [[keep.tile([P, 4, 512], BF16, name="a_raw%d%d" % (g, c)) for c in range(2)] for g in range(2)]
-        ego_raw = [keep.tile([P, 4, EMB], BF16, name="ego_raw%d" % c) for c in range(2)]
-
-        def load_e(c):
-            nc.sync.dma_start(
-                out=e_raw[c][:], in_=e_nodes[512 * c : 512 * (c + 1), :].rearrange("(p j) f -> p j f", j=4)
-            )
-
-        def load_a(g, c):
-            nc.sync.dma_start(
-                out=a_raw[g][c][:],
-                in_=adj[512 * c : 512 * (c + 1), 512 * g : 512 * (g + 1)].rearrange("(p j) e -> p j e", j=4),
-            )
-
-        load_a(0, 0)
-        load_e(0)
-        nc.sync.dma_start(out=gb_rows[0:1, 0:EMB], in_=ln_gamma.unsqueeze(0))
-        nc.sync.dma_start(out=gb_rows[0:1, EMB : 2 * EMB], in_=ln_beta.unsqueeze(0))
-        load_a(0, 1)
-        load_e(1)
-        load_a(1, 0)
-        load_a(1, 1)
-        for c in range(2):
-            nc.sync.dma_start(
-                out=ego_raw[c][:], in_=ego_embeddings[512 * c : 512 * (c + 1), :].rearrange("(p j) f -> p j f", j=4)
-            )
-
+        nc.vector.tensor_copy(out=gb_rows[0:1, :], in_=rows_in[:])
         gamma_b = keep.tile([P, EMB], F32, name="gamma_b")
         beta_b = keep.tile([P, EMB], F32, name="beta_b")
+        for i, dst in enumerate((gamma_b, beta_b)):
+            bc = bank(6 + i, [P, EMB], "bc%d" % i)
+            nc.tensor.matmul(out=bc[:], lhsT=ones[:], rhs=gb_rows[:, EMB * i : EMB * (i + 1)], start=True, stop=True)
+            nc.scalar.copy(out=dst[:], in_=bc[:])
 
-        def spread_gamma_beta():
-            for i, dst in enumerate((gamma_b, beta_b)):
-                bc = bank(i, [P, EMB], "bc%d" % i)
-                nc.tensor.matmul(
-                    out=bc[:], lhsT=ones[:], rhs=gb_rows[:, EMB * i : EMB * (i + 1)], start=True, stop=True
-                )
-                nc.scalar.copy(out=dst[:], in_=bc[:])
-
-        ge = [keep.tile([P, EMB, 4], BF16, name="ge%d" % c, align_bytes=64) for c in range(2)]
-        e_codes = [keep.tile([P, EMB], U32, name="ec%d" % c, align_bytes=64) for c in range(2)]
-        e_scales = [keep.tile([P, EMB], U8, name="es%d" % c, align_bytes=64) for c in range(2)]
-        ga = [[keep.tile([P, 512, 4], BF16, name="ga%d%d" % (g, c), align_bytes=64) for c in range(2)] for g in range(2)]
-        a1_codes = [[keep.tile([P, 512], U32, name="a1c%d%d" % (g, c), align_bytes=64) for c in range(2)] for g in range(2)]
-        a1_scales = [[keep.tile([P, 512], U8, name="a1s%d%d" % (g, c), align_bytes=64) for c in range(2)] for g in range(2)]
-        gb = [[keep.tile([P, 4, P, 2], F32, name="gb%d%d" % (g, c), align_bytes=64) for c in range(2)] for g in range(2)]
-        a2_codes = [[keep.tile([P, 512], U32, name="a2c%d%d" % (g, c), align_bytes=64) for c in range(2)] for g in range(2)]
-        a2_scales = [[keep.tile([P, 512], U8, name="a2s%d%d" % (g, c), align_bytes=64) for c in range(2)] for g in range(2)]
-        gm = [keep.tile([P, EMB, 4], BF16, name="gm%d" % g, align_bytes=64) for g in range(2)]
-        m_codes = [keep.tile([P, EMB], U32, name="mc%d" % g, align_bytes=64) for g in range(2)]
-        m_scales = [keep.tile([P, EMB], U8, name="ms%d" % g, align_bytes=64) for g in range(2)]
+        ge = pair([P, EMB, 4], BF16, "ge")
+        e_codes = pair([P, EMB], U32, "ec")
+        e_scales = pair([P, EMB], U8, "es")
+        ga = grid([P, 512, 4], BF16, "ga")
+        a1_codes = grid([P, 512], U32, "a1c")
+        a1_scales = grid([P, 512], U8, "a1s")
+        gb = grid([P, 4, P, 2], F32, "gb")
+        a2_codes = grid([P, 512], U32, "a2c")
+        a2_scales = grid([P, 512], U8, "a2s")
+        gm = pair([P, EMB, 4], BF16, "gm")
+        m_codes = pair([P, EMB], U32, "mc")
+        m_scales = pair([P, EMB], U8, "ms")
 
         def regroup_e(c):
             nc.vector.tensor_copy(
@@ -115,8 +114,13 @@ def tile_hgnnmodel_pa_kernel(tc, e_nodes, adj, ego_embeddings, ln_gamma, ln_beta
 
         def regroup_a(g, c):
             for u in range(2):
-                src = a_raw[g][c][:, :, 256 * u : 256 * (u + 1)].rearrange("p j (q s) -> p s q j", s=2)
-                dst = ga[g][c][:, 256 * u : 256 * (u + 1), :].rearrange("p (s q) j -> p s q j", s=2)
+                cols = slice(256 * u, 256 * (u + 1))
+                if A_FORM == "write contiguous":
+                    src = a_raw[g][c][:, :, cols].rearrange("p j (q s) -> p s q j", s=2)
+                    dst = ga[g][c][:, cols, :].rearrange("p (s q) j -> p s q j", s=2)
+                else:
+                    src = a_raw[g][c][:, :, cols].rearrange("p j (q s) -> p q j s", s=2)
+                    dst = ga[g][c][:, cols, :].rearrange("p (s q) j -> p q j s", s=2)
                 if u == 1 and (g, c) in A_ON_SCALAR:
                     nc.scalar.copy(out=dst, in_=src)
                 else:
@@ -131,20 +135,13 @@ def tile_hgnnmodel_pa_kernel(tc, e_nodes, adj, ego_embeddings, ln_gamma, ln_beta
 
         def transpose_a(g, c):
             a32 = a_raw[g][c][:].bitcast(F32)
-            banks = []
             for jp in range(2):
                 xt = bank(4 * g + 2 * c + jp, [P, 4, P], "xt%d%d%d" % (g, c, jp))
                 for jj in range(2):
                     for u in range(2):
                         nc.tensor.transpose(xt[:, 2 * jj + u, :], a32[:, 2 * jp + jj, P * u : P * (u + 1)], ident[:])
-                banks.append(xt)
-            return banks
-
-        def copy_xt(g, c, banks):
-            for jp in range(2):
                 nc.scalar.copy(
-                    out=gb[g][c][:, 2 * jp : 2 * jp + 2, :, :],
-                    in_=banks[jp][:].rearrange("q (jj u) n -> q jj n u", u=2),
+                    out=gb[g][c][:, 2 * jp : 2 * jp + 2, :, :], in_=xt[:].rearrange("q (jj u) n -> q jj n u", u=2)
                 )
 
         def quantise_a2(g, c):
@@ -154,39 +151,41 @@ def tile_hgnnmodel_pa_kernel(tc, e_nodes, adj, ego_embeddings, ln_gamma, ln_beta
                 in_=gb[g][c][:].bitcast(BF16).rearrange("q j n w -> q (j n w)"),
             )
 
-        items = (("a", 0, 0), ("e", 0, 0), ("a", 0, 1), ("e", 1, 1), ("a", 1, 0), ("a", 1, 1))
+        def regroup(item):
+            if item[0] == "e":
+                regroup_e(item[1])
+            else:
+                regroup_a(item[1], item[2])
+                transpose_a(item[1], item[2])
 
-        def quantise_item(item):
+        def quantise(item):
             if item[0] == "e":
                 quantise_e(item[1])
             else:
                 quantise_a1(item[1], item[2])
 
-        for i, item in enumerate(items):
-            if item[0] == "e":
-                regroup_e(item[1])
-            else:
-                banks = transpose_a(item[1], item[2])
-                regroup_a(item[1], item[2])
-                copy_xt(item[1], item[2], banks)
-            if i > 0:
-                quantise_item(items[i - 1])
-            if i == 4:
-                spread_gamma_beta()
-        quantise_item(items[-1])
+        for items in ((("a", 0, 0), ("e", 0), ("a", 0, 1), ("e", 1)), (("a", 1, 0), ("a", 1, 1))):
+            for i, item in enumerate(items):
+                regroup(item)
+                if i > 0:
+                    quantise(items[i - 1])
+            quantise(items[-1])
 
         ebs = {}
 
-        def add_beta_on_vector(nt):
+        def add_beta_on_gpsimd(nt):
             c, j = divmod(nt, 4)
             ebs[nt] = keep.tile([P, EMB], F32, name="eb%d" % nt)
-            nc.vector.tensor_tensor(out=ebs[nt][:], in0=ego_raw[c][:, j, :], in1=beta_b[:], op=ALU.add)
+            nc.gpsimd.tensor_tensor(out=ebs[nt][:], in0=ego_raw[c][:, j, :], in1=beta_b[:], op=ALU.add)
 
         def add_beta_on_tensor(nt):
             c, j = divmod(nt, 4)
-            ebs[nt] = bank(nt - EB_ON_VECTOR, [P, EMB], "ebp%d" % nt)
+            ebs[nt] = bank(nt - EB_ON_GPSIMD, [P, EMB], "ebp%d" % nt)
             nc.tensor.matmul(out=ebs[nt][:], lhsT=ident_bf[:], rhs=ego_raw[c][:, j, :], start=True, stop=False)
             nc.tensor.matmul(out=ebs[nt][:], lhsT=ones[:], rhs=gb_rows[:, EMB : 2 * EMB], start=False, stop=True)
+
+        for nt in range(EB_ON_GPSIMD):
+            add_beta_on_gpsimd(nt)
 
         def quantise_m(g, half):
             cols = slice(256 * half, 256 * (half + 1))
@@ -215,9 +214,7 @@ def tile_hgnnmodel_pa_kernel(tc, e_nodes, adj, ego_embeddings, ln_gamma, ln_beta
                 if fc == 1:
                     quantise_a2(g, 1)
                     quantise_m(g, 0)
-                    add_beta_on_vector(g)
             quantise_m(g, 1)
-        add_beta_on_vector(2)
 
         hps = [bank(nt, [P, EMB], "hp%d" % nt) for nt in range(8)]
 
@@ -244,14 +241,12 @@ def tile_hgnnmodel_pa_kernel(tc, e_nodes, adj, ego_embeddings, ln_gamma, ln_beta
         def on_scalar(nt):
             return 0 <= nt < 8 and nt not in STATS_ON_VECTOR
 
-        hsum = {}
-        shift = {}
+        negmean = {}
         ssd = {}
         mv = {}
         for nt in range(8):
             if on_scalar(nt):
-                hsum[nt] = keep.tile([P, 1], F32, name="hsum%d" % nt)
-                shift[nt] = keep.tile([P, 1], F32, name="shift%d" % nt)
+                negmean[nt] = keep.tile([P, 1], F32, name="negmean%d" % nt)
                 ssd[nt] = keep.tile([P, 1], F32, name="ssd%d" % nt)
             else:
                 mv[nt] = keep.tile([P, 2], F32, name="mv%d" % nt)
@@ -259,19 +254,19 @@ def tile_hgnnmodel_pa_kernel(tc, e_nodes, adj, ego_embeddings, ln_gamma, ln_beta
         rstd = [keep.tile([P, 1], F32, name="rstd%d" % nt) for nt in range(8)]
         us = [keep.tile([P, EMB], F32, name="u%d" % nt) for nt in range(8)]
 
-        def row_sums(nt):
+        def minus_mean(nt):
             if on_scalar(nt):
-                nc.scalar.activation(out=junk[:], in_=hps[nt][:], func=ACT.Identity, accum_out=hsum[nt][:])
+                nc.scalar.activation(
+                    out=junk[:], in_=hps[nt][:], func=ACT.Identity, scale=-1.0 / EMB, accum_out=negmean[nt][:]
+                )
 
         for nt in STATS_ON_VECTOR:
-            st6 = small.tile([P, 6], F32, name="st6")
+            st6 = work.tile([P, 6], F32, name="st6")
             nc.vector.bn_stats(out=st6[:], in_=hps[nt][:])
             nc.vector.bn_aggr(out=mv[nt][:], in_=st6[:])
-        row_sums(0)
+        minus_mean(0)
         for k in range(9):
-            if on_scalar(k):
-                nc.scalar.mul(out=shift[k][:], in_=hsum[k][:], mul=-1.0 / EMB)
-            row_sums(k + 1)
+            minus_mean(k + 1)
             if k >= 1:
                 if on_scalar(k - 1):
                     nc.scalar.activation(
@@ -283,25 +278,25 @@ def tile_hgnnmodel_pa_kernel(tc, e_nodes, adj, ego_embeddings, ln_gamma, ln_beta
                     )
             if on_scalar(k):
                 nc.scalar.activation(
-                    out=junk[:], in_=hps[k][:], func=ACT.Square, bias=shift[k][:], accum_out=ssd[k][:]
+                    out=junk[:], in_=hps[k][:], func=ACT.Square, bias=negmean[k][:], accum_out=ssd[k][:]
                 )
             if k >= 1:
                 nc.vector.reciprocal(out=rstd[k - 1][:], in_=std[k - 1][:])
             if k < 8:
                 if on_scalar(k):
                     nc.vector.scalar_tensor_tensor(
-                        out=us[k][:], in0=hps[k][:], scalar=shift[k][:], in1=gamma_b[:], op0=ALU.add, op1=ALU.mult
+                        out=us[k][:], in0=hps[k][:], scalar=negmean[k][:], in1=gamma_b[:], op0=ALU.add, op1=ALU.mult
                     )
                 else:
                     nc.vector.scalar_tensor_tensor(
                         out=us[k][:], in0=hps[k][:], scalar=mv[k][:, 0:1], in1=gamma_b[:],
                         op0=ALU.subtract, op1=ALU.mult,
                     )
-            if EB_ON_VECTOR <= k + EB_ON_VECTOR < 8:
-                add_beta_on_tensor(k + EB_ON_VECTOR)
+            if k + EB_ON_GPSIMD < 8:
+                add_beta_on_tensor(k + EB_ON_GPSIMD)
             if k >= 1:
                 c, j = divmod(k - 1, 4)
-                o_ = work.tile([P, EMB], F32, name="o_", bufs=4)
+                o_ = work.tile([P, EMB], F32, name="o_")
                 nc.vector.scalar_tensor_tensor(
                     out=o_[:], in0=us[k - 1][:], scalar=rstd[k - 1][:], in1=ebs[k - 1][:], op0=ALU.mult, op1=ALU.add
                 )

@@ -83,10 +83,14 @@ def tile_hgnnmodel_pa_kernel(tc, e_nodes, adj, ego_embeddings, ln_gamma, ln_beta
         nc.vector.tensor_copy(out=gb_rows[0:1, :], in_=rows_in[:])
         gamma_b = keep.tile([P, EMB], F32, name="gamma_b")
         beta_b = keep.tile([P, EMB], F32, name="beta_b")
-        for i, dst in enumerate((gamma_b, beta_b)):
-            bc = bank(6 + i, [P, EMB], "bc%d" % i)
-            nc.tensor.matmul(out=bc[:], lhsT=ones[:], rhs=gb_rows[:, EMB * i : EMB * (i + 1)], start=True, stop=True)
-            nc.scalar.copy(out=dst[:], in_=bc[:])
+
+        def spread_gamma_beta():
+            for i, dst in enumerate((gamma_b, beta_b)):
+                bc = bank(i, [P, EMB], "bc%d" % i)
+                nc.tensor.matmul(
+                    out=bc[:], lhsT=ones[:], rhs=gb_rows[:, EMB * i : EMB * (i + 1)], start=True, stop=True
+                )
+                nc.scalar.copy(out=dst[:], in_=bc[:])
 
         ge = pair([P, EMB, 4], BF16, "ge")
         e_codes = pair([P, EMB], U32, "ec")
@@ -170,6 +174,8 @@ def tile_hgnnmodel_pa_kernel(tc, e_nodes, adj, ego_embeddings, ln_gamma, ln_beta
                 if i > 0:
                     quantise(items[i - 1])
             quantise(items[-1])
+            if len(items) == 4:
+                spread_gamma_beta()
 
         ebs = {}
 
@@ -264,6 +270,12 @@ def tile_hgnnmodel_pa_kernel(tc, e_nodes, adj, ego_embeddings, ln_gamma, ln_beta
             st6 = work.tile([P, 6], F32, name="st6")
             nc.vector.bn_stats(out=st6[:], in_=hps[nt][:])
             nc.vector.bn_aggr(out=mv[nt][:], in_=st6[:])
+        late = {}
+
+        def store(nt, tile_):
+            c, j = divmod(nt, 4)
+            nc.sync.dma_start(out=out_v[:, c, j, :], in_=tile_[:])
+
         minus_mean(0)
         for k in range(9):
             minus_mean(k + 1)
@@ -294,10 +306,18 @@ def tile_hgnnmodel_pa_kernel(tc, e_nodes, adj, ego_embeddings, ln_gamma, ln_beta
                     )
             if k + EB_ON_GPSIMD < 8:
                 add_beta_on_tensor(k + EB_ON_GPSIMD)
-            if k >= 1:
-                c, j = divmod(k - 1, 4)
+            if 1 <= k <= EB_ON_GPSIMD:
+                w_ = keep.tile([P, EMB], F32, name="w%d" % (k - 1))
+                nc.gpsimd.tensor_scalar(
+                    out=w_[:], in0=us[k - 1][:], scalar1=rstd[k - 1][:], scalar2=0.0, op0=ALU.mult, op1=ALU.add
+                )
+                late[k - 1] = keep.tile([P, EMB], F32, name="og%d" % (k - 1))
+                nc.gpsimd.tensor_tensor(out=late[k - 1][:], in0=w_[:], in1=ebs[k - 1][:], op=ALU.add)
+            if k > EB_ON_GPSIMD:
                 o_ = work.tile([P, EMB], F32, name="o_")
                 nc.vector.scalar_tensor_tensor(
                     out=o_[:], in0=us[k - 1][:], scalar=rstd[k - 1][:], in1=ebs[k - 1][:], op0=ALU.mult, op1=ALU.add
                 )
-                nc.sync.dma_start(out=out_v[:, c, j, :], in_=o_[:])
+                store(k - 1, o_)
+            if k - 3 in late:
+                store(k - 3, late[k - 3])

@@ -76,21 +76,17 @@ def tile_hgnnmodel_pa_kernel(tc, e_nodes, adj, ego_embeddings, ln_gamma, ln_beta
         ident_bf = keep.tile([P, P], BF16, name="ident_bf")
         make_identity(nc, ident_bf[:])
         warm = keep.tile([P, 1], F32, name="warm")
-        nc.scalar.activation(out=warm[:], in_=one_col[:], func=ACT.Sqrt)
+        nc.scalar.activation(out=warm[:], in_=one_col[:], func=ACT.Abs_reciprocal_sqrt)
         eps_t = keep.tile([P, 1], F32, name="eps_t")
         nc.scalar.mul(out=eps_t[:], in_=one_col[:], mul=LN_EPS)
 
         nc.vector.tensor_copy(out=gb_rows[0:1, :], in_=rows_in[:])
         gamma_b = keep.tile([P, EMB], F32, name="gamma_b")
         beta_b = keep.tile([P, EMB], F32, name="beta_b")
-
-        def spread_gamma_beta():
-            for i, dst in enumerate((gamma_b, beta_b)):
-                bc = bank(i, [P, EMB], "bc%d" % i)
-                nc.tensor.matmul(
-                    out=bc[:], lhsT=ones[:], rhs=gb_rows[:, EMB * i : EMB * (i + 1)], start=True, stop=True
-                )
-                nc.scalar.copy(out=dst[:], in_=bc[:])
+        for i, dst in enumerate((gamma_b, beta_b)):
+            bc = bank(6 + i, [P, EMB], "bc%d" % i)
+            nc.tensor.matmul(out=bc[:], lhsT=ones[:], rhs=gb_rows[:, EMB * i : EMB * (i + 1)], start=True, stop=True)
+            nc.scalar.copy(out=dst[:], in_=bc[:])
 
         ge = pair([P, EMB, 4], BF16, "ge")
         e_codes = pair([P, EMB], U32, "ec")
@@ -174,8 +170,6 @@ def tile_hgnnmodel_pa_kernel(tc, e_nodes, adj, ego_embeddings, ln_gamma, ln_beta
                 if i > 0:
                     quantise(items[i - 1])
             quantise(items[-1])
-            if len(items) == 4:
-                spread_gamma_beta()
 
         ebs = {}
 
@@ -256,7 +250,6 @@ def tile_hgnnmodel_pa_kernel(tc, e_nodes, adj, ego_embeddings, ln_gamma, ln_beta
                 ssd[nt] = keep.tile([P, 1], F32, name="ssd%d" % nt)
             else:
                 mv[nt] = keep.tile([P, 2], F32, name="mv%d" % nt)
-        std = [keep.tile([P, 1], F32, name="std%d" % nt) for nt in range(8)]
         rstd = [keep.tile([P, 1], F32, name="rstd%d" % nt) for nt in range(8)]
         us = [keep.tile([P, EMB], F32, name="u%d" % nt) for nt in range(8)]
 
@@ -270,30 +263,24 @@ def tile_hgnnmodel_pa_kernel(tc, e_nodes, adj, ego_embeddings, ln_gamma, ln_beta
             st6 = work.tile([P, 6], F32, name="st6")
             nc.vector.bn_stats(out=st6[:], in_=hps[nt][:])
             nc.vector.bn_aggr(out=mv[nt][:], in_=st6[:])
-        late = {}
-
-        def store(nt, tile_):
-            c, j = divmod(nt, 4)
-            nc.sync.dma_start(out=out_v[:, c, j, :], in_=tile_[:])
-
         minus_mean(0)
         for k in range(9):
             minus_mean(k + 1)
             if k >= 1:
                 if on_scalar(k - 1):
                     nc.scalar.activation(
-                        out=std[k - 1][:], in_=ssd[k - 1][:], func=ACT.Sqrt, bias=eps_t[:], scale=1.0 / EMB
+                        out=rstd[k - 1][:], in_=ssd[k - 1][:], func=ACT.Abs_reciprocal_sqrt, bias=eps_t[:],
+                        scale=1.0 / EMB,
                     )
                 else:
                     nc.scalar.activation(
-                        out=std[k - 1][:], in_=mv[k - 1][:, 1:2], func=ACT.Sqrt, bias=eps_t[:], scale=1.0
+                        out=rstd[k - 1][:], in_=mv[k - 1][:, 1:2], func=ACT.Abs_reciprocal_sqrt, bias=eps_t[:],
+                        scale=1.0,
                     )
             if on_scalar(k):
                 nc.scalar.activation(
                     out=junk[:], in_=hps[k][:], func=ACT.Square, bias=negmean[k][:], accum_out=ssd[k][:]
                 )
-            if k >= 1:
-                nc.vector.reciprocal(out=rstd[k - 1][:], in_=std[k - 1][:])
             if k < 8:
                 if on_scalar(k):
                     nc.vector.scalar_tensor_tensor(
@@ -306,18 +293,10 @@ def tile_hgnnmodel_pa_kernel(tc, e_nodes, adj, ego_embeddings, ln_gamma, ln_beta
                     )
             if k + EB_ON_GPSIMD < 8:
                 add_beta_on_tensor(k + EB_ON_GPSIMD)
-            if 1 <= k <= EB_ON_GPSIMD:
-                w_ = keep.tile([P, EMB], F32, name="w%d" % (k - 1))
-                nc.gpsimd.tensor_scalar(
-                    out=w_[:], in0=us[k - 1][:], scalar1=rstd[k - 1][:], scalar2=0.0, op0=ALU.mult, op1=ALU.add
-                )
-                late[k - 1] = keep.tile([P, EMB], F32, name="og%d" % (k - 1))
-                nc.gpsimd.tensor_tensor(out=late[k - 1][:], in0=w_[:], in1=ebs[k - 1][:], op=ALU.add)
-            if k > EB_ON_GPSIMD:
+            if k >= 1:
+                c, j = divmod(k - 1, 4)
                 o_ = work.tile([P, EMB], F32, name="o_")
                 nc.vector.scalar_tensor_tensor(
                     out=o_[:], in0=us[k - 1][:], scalar=rstd[k - 1][:], in1=ebs[k - 1][:], op0=ALU.mult, op1=ALU.add
                 )
-                store(k - 1, o_)
-            if k - 3 in late:
-                store(k - 3, late[k - 3])
+                nc.sync.dma_start(out=out_v[:, c, j, :], in_=o_[:])

@@ -19,7 +19,7 @@ FLOPS = 2 * 2 * 1024 * 1024 * 512
 
 A_ON_SCALAR = ((0, 1), (1, 0))
 STATS_ON_VECTOR = (0, 2)
-EB_ON_GPSIMD = 3
+EB_ON_TENSOR = 6
 A_FORM = "write contiguous"
 
 
@@ -43,7 +43,8 @@ def tile_hgnnmodel_pa_kernel(tc, e_nodes, adj, ego_embeddings, ln_gamma, ln_beta
         def pair(shape, dtype, name):
             return [keep.tile(shape, dtype, name="%s%d" % (name, i), align_bytes=64) for i in range(2)]
 
-        rows_in = keep.tile([1, 2 * EMB], BF16, name="rows_in")
+        gamma_b = keep.tile([P, EMB], BF16, name="gamma_b")
+        beta_b = keep.tile([P, EMB], BF16, name="beta_b")
         e_raw = pair([P, 4, EMB], BF16, "e_raw")
         a_raw = grid([P, 4, 512], BF16, "a_raw")
         ego_raw = pair([P, 4, EMB], BF16, "ego_raw")
@@ -54,8 +55,6 @@ def tile_hgnnmodel_pa_kernel(tc, e_nodes, adj, ego_embeddings, ln_gamma, ln_beta
         def load_a(g, c):
             load_rows(a_raw[g][c], adj[:, 512 * g : 512 * (g + 1)], c)
 
-        nc.sync.dma_start(out=rows_in[:, 0:EMB], in_=ln_gamma.unsqueeze(0))
-        nc.sync.dma_start(out=rows_in[:, EMB : 2 * EMB], in_=ln_beta.unsqueeze(0))
         load_a(0, 0)
         load_rows(e_raw[0], e_nodes, 0)
         load_a(0, 1)
@@ -64,11 +63,9 @@ def tile_hgnnmodel_pa_kernel(tc, e_nodes, adj, ego_embeddings, ln_gamma, ln_beta
         load_a(1, 1)
         load_rows(ego_raw[0], ego_embeddings, 0)
         load_rows(ego_raw[1], ego_embeddings, 1)
+        nc.sync.dma_start(out=beta_b[:], in_=ln_beta.partition_broadcast(P))
+        nc.sync.dma_start(out=gamma_b[:], in_=ln_gamma.partition_broadcast(P))
 
-        gb_rows = keep.tile([P, 2 * EMB], BF16, name="gb_rows")
-        nc.vector.memset(gb_rows[:].bitcast(I32), 0)
-        ones = keep.tile([P, P], BF16, name="ones")
-        nc.vector.memset(ones[:], 1.0)
         one_col = keep.tile([P, 1], F32, name="one_col")
         nc.vector.memset(one_col[:], 1.0)
         ident = keep.tile([P, P], F32, name="ident")
@@ -79,14 +76,6 @@ def tile_hgnnmodel_pa_kernel(tc, e_nodes, adj, ego_embeddings, ln_gamma, ln_beta
         nc.scalar.activation(out=warm[:], in_=one_col[:], func=ACT.Abs_reciprocal_sqrt)
         eps_t = keep.tile([P, 1], F32, name="eps_t")
         nc.scalar.mul(out=eps_t[:], in_=one_col[:], mul=LN_EPS)
-
-        nc.vector.tensor_copy(out=gb_rows[0:1, :], in_=rows_in[:])
-        gamma_b = keep.tile([P, EMB], F32, name="gamma_b")
-        beta_b = keep.tile([P, EMB], F32, name="beta_b")
-        for i, dst in enumerate((gamma_b, beta_b)):
-            bc = bank(6 + i, [P, EMB], "bc%d" % i)
-            nc.tensor.matmul(out=bc[:], lhsT=ones[:], rhs=gb_rows[:, EMB * i : EMB * (i + 1)], start=True, stop=True)
-            nc.scalar.copy(out=dst[:], in_=bc[:])
 
         ge = pair([P, EMB, 4], BF16, "ge")
         e_codes = pair([P, EMB], U32, "ec")
@@ -180,12 +169,9 @@ def tile_hgnnmodel_pa_kernel(tc, e_nodes, adj, ego_embeddings, ln_gamma, ln_beta
 
         def add_beta_on_tensor(nt):
             c, j = divmod(nt, 4)
-            ebs[nt] = bank(nt - EB_ON_GPSIMD, [P, EMB], "ebp%d" % nt)
+            ebs[nt] = bank(6 + nt % 2, [P, EMB], "ebp%d" % nt)
             nc.tensor.matmul(out=ebs[nt][:], lhsT=ident_bf[:], rhs=ego_raw[c][:, j, :], start=True, stop=False)
-            nc.tensor.matmul(out=ebs[nt][:], lhsT=ones[:], rhs=gb_rows[:, EMB : 2 * EMB], start=False, stop=True)
-
-        for nt in range(EB_ON_GPSIMD):
-            add_beta_on_gpsimd(nt)
+            nc.tensor.matmul(out=ebs[nt][:], lhsT=ident_bf[:], rhs=beta_b[:], start=False, stop=True)
 
         def quantise_m(g, half):
             cols = slice(256 * half, 256 * (half + 1))
@@ -216,10 +202,12 @@ def tile_hgnnmodel_pa_kernel(tc, e_nodes, adj, ego_embeddings, ln_gamma, ln_beta
                     quantise_m(g, 0)
             quantise_m(g, 1)
 
-        hps = [bank(nt, [P, EMB], "hp%d" % nt) for nt in range(8)]
+        hps = {}
 
         def second_matmul(nt, g):
             c, j = divmod(nt, 4)
+            if g == 0:
+                hps[nt] = bank(nt % 6, [P, EMB], "hp%d" % nt)
             nc.tensor.matmul_mx(
                 out=hps[nt][:],
                 lhsT=a2_codes[g][c][:, P * j : P * (j + 1)].bitcast(FP8X4),
@@ -230,10 +218,15 @@ def tile_hgnnmodel_pa_kernel(tc, e_nodes, adj, ego_embeddings, ln_gamma, ln_beta
                 stop=(g == 1),
             )
 
-        for half in range(2):
-            for g in range(2):
-                for nt in range(4 * half, 4 * half + 4):
-                    second_matmul(nt, g)
+        for nt in range(4):
+            second_matmul(nt, 0)
+        add_beta_on_tensor(0)
+        for nt in range(4):
+            second_matmul(nt, 1)
+        for nt in range(4, 6):
+            second_matmul(nt, 0)
+            second_matmul(nt, 1)
+        add_beta_on_tensor(1)
 
         out_v = out.rearrange("(c p j) f -> p c j f", c=2, j=4)
         junk = keep.tile([P, EMB], BF16, name="junk")
@@ -264,8 +257,13 @@ def tile_hgnnmodel_pa_kernel(tc, e_nodes, adj, ego_embeddings, ln_gamma, ln_beta
             nc.vector.bn_stats(out=st6[:], in_=hps[nt][:])
             nc.vector.bn_aggr(out=mv[nt][:], in_=st6[:])
         minus_mean(0)
+        started = keep.tile([P, 1], F32, name="started")
         for k in range(9):
             minus_mean(k + 1)
+            if k == 0:
+                nc.gpsimd.tensor_copy(out=started[:], in_=negmean[1][:])
+                for nt in range(EB_ON_TENSOR, 8):
+                    add_beta_on_gpsimd(nt)
             if k >= 1:
                 if on_scalar(k - 1):
                     nc.scalar.activation(
@@ -291,8 +289,9 @@ def tile_hgnnmodel_pa_kernel(tc, e_nodes, adj, ego_embeddings, ln_gamma, ln_beta
                         out=us[k][:], in0=hps[k][:], scalar=mv[k][:, 0:1], in1=gamma_b[:],
                         op0=ALU.subtract, op1=ALU.mult,
                     )
-            if k + EB_ON_GPSIMD < 8:
-                add_beta_on_tensor(k + EB_ON_GPSIMD)
+            if k < 2:
+                second_matmul(k + 6, 0)
+                second_matmul(k + 6, 1)
             if k >= 1:
                 c, j = divmod(k - 1, 4)
                 o_ = work.tile([P, EMB], F32, name="o_")
@@ -300,3 +299,5 @@ def tile_hgnnmodel_pa_kernel(tc, e_nodes, adj, ego_embeddings, ln_gamma, ln_beta
                     out=o_[:], in0=us[k - 1][:], scalar=rstd[k - 1][:], in1=ebs[k - 1][:], op0=ALU.mult, op1=ALU.add
                 )
                 nc.sync.dma_start(out=out_v[:, c, j, :], in_=o_[:])
+                if k + 1 < EB_ON_TENSOR:
+                    add_beta_on_tensor(k + 1)

@@ -20,7 +20,6 @@ FLOPS = 2 * 2 * 1024 * 1024 * 512
 A_ON_SCALAR = ((0, 1), (1, 0))
 STATS_ON_VECTOR = (0, 2)
 EB_ON_TENSOR = 6
-A_FORM = "write contiguous"
 
 
 def tile_hgnnmodel_pa_kernel(tc, e_nodes, adj, ego_embeddings, ln_gamma, ln_beta, out):
@@ -104,12 +103,8 @@ def tile_hgnnmodel_pa_kernel(tc, e_nodes, adj, ego_embeddings, ln_gamma, ln_beta
         def regroup_a(g, c):
             for u in range(2):
                 cols = slice(256 * u, 256 * (u + 1))
-                if A_FORM == "write contiguous":
-                    src = a_raw[g][c][:, :, cols].rearrange("p j (q s) -> p s q j", s=2)
-                    dst = ga[g][c][:, cols, :].rearrange("p (s q) j -> p s q j", s=2)
-                else:
-                    src = a_raw[g][c][:, :, cols].rearrange("p j (q s) -> p q j s", s=2)
-                    dst = ga[g][c][:, cols, :].rearrange("p (s q) j -> p q j s", s=2)
+                src = a_raw[g][c][:, :, cols].rearrange("p j (b r s) -> p b j r s", r=2, s=2)
+                dst = ga[g][c][:, cols, :].rearrange("p (s b r) j -> p b j r s", s=2, r=2)
                 if u == 1 and (g, c) in A_ON_SCALAR:
                     nc.scalar.copy(out=dst, in_=src)
                 else:

@@ -18,15 +18,17 @@ LN_EPS = 1e-5
 FLOPS = 2 * 2 * 1024 * 1024 * 512
 
 A_ON_SCALAR = ((0, 1), (1, 0))
-STATS_ON_VECTOR = (0, 2)
-EB_ON_TENSOR = 6
+STATS_ON_VECTOR = (0, 2, 6)
+FINISH_ON_GPSIMD = (2, 4)
+EB_ON_TENSOR = (0, 1, 3, 5, 6, 7)
+EB_BANKS = (6, 7, 2, 6, 7, 2)
 
 
 def tile_hgnnmodel_pa_kernel(tc, e_nodes, adj, ego_embeddings, ln_gamma, ln_beta, out):
     nc = tc.nc
     with ExitStack() as ctx:
         keep = ctx.enter_context(tc.tile_pool(name="keep", bufs=1))
-        work = ctx.enter_context(tc.tile_pool(name="work", bufs=4))
+        work = ctx.enter_context(tc.tile_pool(name="work", bufs=8))
         psum = ctx.enter_context(tc.psum_pool(name="psum", bufs=1))
         ctx.enter_context(tc.manual_schedule())
 
@@ -164,7 +166,7 @@ def tile_hgnnmodel_pa_kernel(tc, e_nodes, adj, ego_embeddings, ln_gamma, ln_beta
 
         def add_beta_on_tensor(nt):
             c, j = divmod(nt, 4)
-            ebs[nt] = bank(6 + nt % 2, [P, EMB], "ebp%d" % nt)
+            ebs[nt] = bank(EB_BANKS[EB_ON_TENSOR.index(nt)], [P, EMB], "ebp%d" % nt)
             nc.tensor.matmul(out=ebs[nt][:], lhsT=ident_bf[:], rhs=ego_raw[c][:, j, :], start=True, stop=False)
             nc.tensor.matmul(out=ebs[nt][:], lhsT=ident_bf[:], rhs=beta_b[:], start=False, stop=True)
 
@@ -215,13 +217,13 @@ def tile_hgnnmodel_pa_kernel(tc, e_nodes, adj, ego_embeddings, ln_gamma, ln_beta
 
         for nt in range(4):
             second_matmul(nt, 0)
-        add_beta_on_tensor(0)
+        add_beta_on_tensor(EB_ON_TENSOR[0])
         for nt in range(4):
             second_matmul(nt, 1)
         for nt in range(4, 6):
             second_matmul(nt, 0)
             second_matmul(nt, 1)
-        add_beta_on_tensor(1)
+        add_beta_on_tensor(EB_ON_TENSOR[1])
 
         out_v = out.rearrange("(c p j) f -> p c j f", c=2, j=4)
         junk = keep.tile([P, EMB], BF16, name="junk")
@@ -247,17 +249,20 @@ def tile_hgnnmodel_pa_kernel(tc, e_nodes, adj, ego_embeddings, ln_gamma, ln_beta
                     out=junk[:], in_=hps[nt][:], func=ACT.Identity, scale=-1.0 / EMB, accum_out=negmean[nt][:]
                 )
 
-        for nt in STATS_ON_VECTOR:
+        def vector_stats(nt):
             st6 = work.tile([P, 6], F32, name="st6")
             nc.vector.bn_stats(out=st6[:], in_=hps[nt][:])
             nc.vector.bn_aggr(out=mv[nt][:], in_=st6[:])
-        minus_mean(0)
+
+        vector_stats(0)
+        vector_stats(2)
+        late_stores = []
         started = keep.tile([P, 1], F32, name="started")
         for k in range(9):
             minus_mean(k + 1)
             if k == 0:
                 nc.gpsimd.tensor_copy(out=started[:], in_=negmean[1][:])
-                for nt in range(EB_ON_TENSOR, 8):
+                for nt in FINISH_ON_GPSIMD:
                     add_beta_on_gpsimd(nt)
             if k >= 1:
                 if on_scalar(k - 1):
@@ -284,15 +289,31 @@ def tile_hgnnmodel_pa_kernel(tc, e_nodes, adj, ego_embeddings, ln_gamma, ln_beta
                         out=us[k][:], in0=hps[k][:], scalar=mv[k][:, 0:1], in1=gamma_b[:],
                         op0=ALU.subtract, op1=ALU.mult,
                     )
+            if k > 1 and k + 1 in STATS_ON_VECTOR:
+                vector_stats(k + 1)
             if k < 2:
                 second_matmul(k + 6, 0)
                 second_matmul(k + 6, 1)
+            if k == 2:
+                add_beta_on_tensor(EB_ON_TENSOR[2])
             if k >= 1:
+                if k - 3 in FINISH_ON_GPSIMD:
+                    late, c, j = late_stores[FINISH_ON_GPSIMD.index(k - 3)]
+                    nc.sync.dma_start(out=out_v[:, c, j, :], in_=late[:])
                 c, j = divmod(k - 1, 4)
                 o_ = work.tile([P, EMB], F32, name="o_")
-                nc.vector.scalar_tensor_tensor(
-                    out=o_[:], in0=us[k - 1][:], scalar=rstd[k - 1][:], in1=ebs[k - 1][:], op0=ALU.mult, op1=ALU.add
-                )
-                nc.sync.dma_start(out=out_v[:, c, j, :], in_=o_[:])
-                if k + 1 < EB_ON_TENSOR:
-                    add_beta_on_tensor(k + 1)
+                if k - 1 in FINISH_ON_GPSIMD:
+                    scaled = work.tile([P, EMB], F32, name="scaled")
+                    nc.gpsimd.tensor_scalar(
+                        out=scaled[:], in0=us[k - 1][:], scalar1=rstd[k - 1][:], scalar2=0.0, op0=ALU.mult, op1=ALU.add
+                    )
+                    nc.gpsimd.tensor_tensor(out=o_[:], in0=scaled[:], in1=ebs[k - 1][:], op=ALU.add)
+                    late_stores.append((o_, c, j))
+                else:
+                    nc.vector.scalar_tensor_tensor(
+                        out=o_[:], in0=us[k - 1][:], scalar=rstd[k - 1][:], in1=ebs[k - 1][:], op0=ALU.mult, op1=ALU.add
+                    )
+                    nc.sync.dma_start(out=out_v[:, c, j, :], in_=o_[:])
+                    i = EB_ON_TENSOR.index(k - 1) + 2
+                    if 3 <= i < len(EB_ON_TENSOR):
+                        add_beta_on_tensor(EB_ON_TENSOR[i])

@@ -17,11 +17,13 @@ EMB = 512
 LN_EPS = 1e-5
 FLOPS = 2 * 2 * 1024 * 1024 * 512
 
-A_ON_SCALAR = ((0, 1), (1, 0))
-STATS_ON_VECTOR = (0, 2, 6)
+XT_BANKS = ((0, 2), (4, 6))
+MP_BANKS = ((0, 1, 2, 3), (4, 5, 6, 7))
+HP_BANKS = (0, 1, 2, 3, 4, 5, 0, 1)
+EB_BANKS = (6, 7, 2, 6, 7, 2)
+STATS_ON_VECTOR = (0, 2, 5)
 FINISH_ON_GPSIMD = (2, 4)
 EB_ON_TENSOR = (0, 1, 3, 5, 6, 7)
-EB_BANKS = (6, 7, 2, 6, 7, 2)
 
 
 def tile_hgnnmodel_pa_kernel(tc, e_nodes, adj, ego_embeddings, ln_gamma, ln_beta, out):
@@ -102,33 +104,37 @@ def tile_hgnnmodel_pa_kernel(tc, e_nodes, adj, ego_embeddings, ln_gamma, ln_beta
                 out=e_codes[c][:].bitcast(FP8X4), scales=e_scales[c][:], in_=ge[c][:].rearrange("p w j -> p (w j)")
             )
 
-        def regroup_a(g, c):
-            for u in range(2):
-                cols = slice(256 * u, 256 * (u + 1))
-                src = a_raw[g][c][:, :, cols].rearrange("p j (b r s) -> p b j r s", r=2, s=2)
-                dst = ga[g][c][:, cols, :].rearrange("p (s b r) j -> p b j r s", s=2, r=2)
-                if u == 1 and (g, c) in A_ON_SCALAR:
-                    nc.scalar.copy(out=dst, in_=src)
-                else:
-                    nc.vector.tensor_copy(out=dst, in_=src)
-
-        def quantise_a1(g, c):
-            nc.vector.quantize_mx(
-                out=a1_codes[g][c][:].bitcast(FP8X4),
-                scales=a1_scales[g][c][:],
-                in_=ga[g][c][:].rearrange("p w j -> p (w j)"),
+        def regroup_a(engine_copy, g, c, u):
+            cols = slice(256 * u, 256 * (u + 1))
+            engine_copy(
+                out=ga[g][c][:, cols, :].rearrange("p (s b r) j -> p b j r s", s=2, r=2),
+                in_=a_raw[g][c][:, :, cols].rearrange("p j (b r s) -> p b j r s", r=2, s=2),
             )
+
+        def quantise_a1(g, c, cols=slice(0, 512)):
+            nc.vector.quantize_mx(
+                out=a1_codes[g][c][:, cols].bitcast(FP8X4),
+                scales=a1_scales[g][c][:, cols],
+                in_=ga[g][c][:, cols, :].rearrange("p w j -> p (w j)"),
+            )
+
+        xts = {}
 
         def transpose_a(g, c):
             a32 = a_raw[g][c][:].bitcast(F32)
             for jp in range(2):
-                xt = bank(4 * g + 2 * c + jp, [P, 4, P], "xt%d%d%d" % (g, c, jp))
+                xts[g, c, jp] = bank(XT_BANKS[g][c] + jp, [P, 4, P], "xt%d%d%d" % (g, c, jp))
                 for jj in range(2):
                     for u in range(2):
-                        nc.tensor.transpose(xt[:, 2 * jj + u, :], a32[:, 2 * jp + jj, P * u : P * (u + 1)], ident[:])
-                nc.scalar.copy(
-                    out=gb[g][c][:, 2 * jp : 2 * jp + 2, :, :], in_=xt[:].rearrange("q (jj u) n -> q jj n u", u=2)
-                )
+                        nc.tensor.transpose(
+                            xts[g, c, jp][:, 2 * jj + u, :], a32[:, 2 * jp + jj, P * u : P * (u + 1)], ident[:]
+                        )
+
+        def copy_words(g, c, jp):
+            nc.scalar.copy(
+                out=gb[g][c][:, 2 * jp : 2 * jp + 2, :, :],
+                in_=xts[g, c, jp][:].rearrange("q (jj u) n -> q jj n u", u=2),
+            )
 
         def quantise_a2(g, c):
             nc.vector.quantize_mx(
@@ -136,26 +142,6 @@ def tile_hgnnmodel_pa_kernel(tc, e_nodes, adj, ego_embeddings, ln_gamma, ln_beta
                 scales=a2_scales[g][c][:],
                 in_=gb[g][c][:].bitcast(BF16).rearrange("q j n w -> q (j n w)"),
             )
-
-        def regroup(item):
-            if item[0] == "e":
-                regroup_e(item[1])
-            else:
-                regroup_a(item[1], item[2])
-                transpose_a(item[1], item[2])
-
-        def quantise(item):
-            if item[0] == "e":
-                quantise_e(item[1])
-            else:
-                quantise_a1(item[1], item[2])
-
-        for items in ((("a", 0, 0), ("e", 0), ("a", 0, 1), ("e", 1)), (("a", 1, 0), ("a", 1, 1))):
-            for i, item in enumerate(items):
-                regroup(item)
-                if i > 0:
-                    quantise(items[i - 1])
-            quantise(items[-1])
 
         ebs = {}
 
@@ -170,6 +156,27 @@ def tile_hgnnmodel_pa_kernel(tc, e_nodes, adj, ego_embeddings, ln_gamma, ln_beta
             nc.tensor.matmul(out=ebs[nt][:], lhsT=ident_bf[:], rhs=ego_raw[c][:, j, :], start=True, stop=False)
             nc.tensor.matmul(out=ebs[nt][:], lhsT=ident_bf[:], rhs=beta_b[:], start=False, stop=True)
 
+        mps = {}
+
+        def first_matmul(g, fcs, ts):
+            for fc in fcs:
+                if ts[0] == 0:
+                    mps[g, fc] = bank(MP_BANKS[g][fc], [P, 4, P], "mp%d%d" % (g, fc))
+                for t in ts:
+                    for c in range(2):
+                        nc.tensor.matmul_mx(
+                            out=mps[g, fc][:, t, :],
+                            lhsT=a1_codes[g][c][:, P * t : P * (t + 1)].bitcast(FP8X4),
+                            lhsT_scale=a1_scales[g][c][:, P * t : P * (t + 1)],
+                            rhs=e_codes[c][:, P * fc : P * (fc + 1)].bitcast(FP8X4),
+                            rhs_scale=e_scales[c][:, P * fc : P * (fc + 1)],
+                            start=(c == 0),
+                            stop=(c == 1),
+                        )
+
+        def copy_m(engine_copy, g, fc):
+            engine_copy(out=gm[g][:, P * fc : P * (fc + 1), :], in_=mps[g, fc][:].rearrange("p t f -> p f t"))
+
         def quantise_m(g, half):
             cols = slice(256 * half, 256 * (half + 1))
             nc.vector.quantize_mx(
@@ -178,33 +185,12 @@ def tile_hgnnmodel_pa_kernel(tc, e_nodes, adj, ego_embeddings, ln_gamma, ln_beta
                 in_=gm[g][:, cols, :].rearrange("p w j -> p (w j)"),
             )
 
-        for g in range(2):
-            quantise_a2(g, 0)
-            for fc in range(4):
-                mp = bank(4 * g + fc, [P, 4, P], "mp%d%d" % (g, fc))
-                for t in range(4):
-                    for c in range(2):
-                        nc.tensor.matmul_mx(
-                            out=mp[:, t, :],
-                            lhsT=a1_codes[g][c][:, P * t : P * (t + 1)].bitcast(FP8X4),
-                            lhsT_scale=a1_scales[g][c][:, P * t : P * (t + 1)],
-                            rhs=e_codes[c][:, P * fc : P * (fc + 1)].bitcast(FP8X4),
-                            rhs_scale=e_scales[c][:, P * fc : P * (fc + 1)],
-                            start=(c == 0),
-                            stop=(c == 1),
-                        )
-                nc.scalar.copy(out=gm[g][:, P * fc : P * (fc + 1), :], in_=mp[:].rearrange("p t f -> p f t"))
-                if fc == 1:
-                    quantise_a2(g, 1)
-                    quantise_m(g, 0)
-            quantise_m(g, 1)
-
         hps = {}
 
         def second_matmul(nt, g):
             c, j = divmod(nt, 4)
             if g == 0:
-                hps[nt] = bank(nt % 6, [P, EMB], "hp%d" % nt)
+                hps[nt] = bank(HP_BANKS[nt], [P, EMB], "hp%d" % nt)
             nc.tensor.matmul_mx(
                 out=hps[nt][:],
                 lhsT=a2_codes[g][c][:, P * j : P * (j + 1)].bitcast(FP8X4),
@@ -215,6 +201,52 @@ def tile_hgnnmodel_pa_kernel(tc, e_nodes, adj, ego_embeddings, ln_gamma, ln_beta
                 stop=(g == 1),
             )
 
+        vector_copy = nc.vector.tensor_copy
+        scalar_copy = nc.scalar.copy
+
+        every = range(4)
+        regroup_a(vector_copy, 0, 0, 0)
+        regroup_a(vector_copy, 0, 0, 1)
+        transpose_a(0, 0)
+        copy_words(0, 0, 0)
+        copy_words(0, 0, 1)
+        regroup_e(0)
+        quantise_a1(0, 0)
+        regroup_a(vector_copy, 0, 1, 0)
+        regroup_a(scalar_copy, 0, 1, 1)
+        transpose_a(0, 1)
+        copy_words(0, 1, 0)
+        copy_words(0, 1, 1)
+        quantise_e(0)
+        regroup_e(1)
+        quantise_a1(0, 1)
+        quantise_e(1)
+        regroup_a(vector_copy, 1, 0, 0)
+        regroup_a(scalar_copy, 1, 0, 1)
+        transpose_a(1, 0)
+        copy_words(1, 0, 0)
+        copy_words(1, 0, 1)
+        regroup_a(vector_copy, 1, 1, 0)
+        regroup_a(vector_copy, 1, 1, 1)
+        transpose_a(1, 1)
+        copy_words(1, 1, 0)
+        copy_words(1, 1, 1)
+        quantise_a1(1, 0)
+        quantise_a1(1, 1)
+        first_matmul(0, every, every)
+        for fc in every:
+            copy_m(scalar_copy, 0, fc)
+        quantise_a2(0, 0)
+        quantise_a2(0, 1)
+        quantise_m(0, 0)
+        quantise_m(0, 1)
+        first_matmul(1, every, every)
+        for fc in every:
+            copy_m(scalar_copy, 1, fc)
+        quantise_a2(1, 0)
+        quantise_a2(1, 1)
+        quantise_m(1, 0)
+        quantise_m(1, 1)
         for nt in range(4):
             second_matmul(nt, 0)
         add_beta_on_tensor(EB_ON_TENSOR[0])
@@ -254,41 +286,62 @@ def tile_hgnnmodel_pa_kernel(tc, e_nodes, adj, ego_embeddings, ln_gamma, ln_beta
             nc.vector.bn_stats(out=st6[:], in_=hps[nt][:])
             nc.vector.bn_aggr(out=mv[nt][:], in_=st6[:])
 
+        def squares(nt):
+            if on_scalar(nt):
+                nc.scalar.activation(
+                    out=junk[:], in_=hps[nt][:], func=ACT.Square, bias=negmean[nt][:], accum_out=ssd[nt][:]
+                )
+
+        def inverse_deviation(nt):
+            variance, scale = (ssd[nt][:], 1.0 / EMB) if on_scalar(nt) else (mv[nt][:, 1:2], 1.0)
+            nc.scalar.activation(
+                out=rstd[nt][:], in_=variance, func=ACT.Abs_reciprocal_sqrt, bias=eps_t[:], scale=scale
+            )
+
+        def times_gamma(nt):
+            if on_scalar(nt):
+                nc.vector.scalar_tensor_tensor(
+                    out=us[nt][:], in0=hps[nt][:], scalar=negmean[nt][:], in1=gamma_b[:], op0=ALU.add, op1=ALU.mult
+                )
+            else:
+                nc.vector.scalar_tensor_tensor(
+                    out=us[nt][:], in0=hps[nt][:], scalar=mv[nt][:, 0:1], in1=gamma_b[:],
+                    op0=ALU.subtract, op1=ALU.mult,
+                )
+
+        finished = {}
+
+        def finish(nt):
+            o_ = work.tile([P, EMB], F32, name="o_")
+            if nt in FINISH_ON_GPSIMD:
+                scaled = work.tile([P, EMB], F32, name="scaled")
+                nc.gpsimd.tensor_scalar(
+                    out=scaled[:], in0=us[nt][:], scalar1=rstd[nt][:], scalar2=0.0, op0=ALU.mult, op1=ALU.add
+                )
+                nc.gpsimd.tensor_tensor(out=o_[:], in0=scaled[:], in1=ebs[nt][:], op=ALU.add)
+            else:
+                nc.vector.scalar_tensor_tensor(
+                    out=o_[:], in0=us[nt][:], scalar=rstd[nt][:], in1=ebs[nt][:], op0=ALU.mult, op1=ALU.add
+                )
+            finished[nt] = o_
+
+        def store(nt):
+            c, j = divmod(nt, 4)
+            nc.sync.dma_start(out=out_v[:, c, j, :], in_=finished[nt][:])
+
+        started = keep.tile([P, 1], U32, name="started")
+        nc.gpsimd.tensor_copy(out=started[:], in_=m_codes[1][:, EMB - 1 : EMB])
+        for nt in FINISH_ON_GPSIMD[:2]:
+            add_beta_on_gpsimd(nt)
         vector_stats(0)
         vector_stats(2)
-        late_stores = []
-        started = keep.tile([P, 1], F32, name="started")
         for k in range(9):
             minus_mean(k + 1)
-            if k == 0:
-                nc.gpsimd.tensor_copy(out=started[:], in_=negmean[1][:])
-                for nt in FINISH_ON_GPSIMD:
-                    add_beta_on_gpsimd(nt)
             if k >= 1:
-                if on_scalar(k - 1):
-                    nc.scalar.activation(
-                        out=rstd[k - 1][:], in_=ssd[k - 1][:], func=ACT.Abs_reciprocal_sqrt, bias=eps_t[:],
-                        scale=1.0 / EMB,
-                    )
-                else:
-                    nc.scalar.activation(
-                        out=rstd[k - 1][:], in_=mv[k - 1][:, 1:2], func=ACT.Abs_reciprocal_sqrt, bias=eps_t[:],
-                        scale=1.0,
-                    )
-            if on_scalar(k):
-                nc.scalar.activation(
-                    out=junk[:], in_=hps[k][:], func=ACT.Square, bias=negmean[k][:], accum_out=ssd[k][:]
-                )
+                inverse_deviation(k - 1)
+            squares(k)
             if k < 8:
-                if on_scalar(k):
-                    nc.vector.scalar_tensor_tensor(
-                        out=us[k][:], in0=hps[k][:], scalar=negmean[k][:], in1=gamma_b[:], op0=ALU.add, op1=ALU.mult
-                    )
-                else:
-                    nc.vector.scalar_tensor_tensor(
-                        out=us[k][:], in0=hps[k][:], scalar=mv[k][:, 0:1], in1=gamma_b[:],
-                        op0=ALU.subtract, op1=ALU.mult,
-                    )
+                times_gamma(k)
             if k > 1 and k + 1 in STATS_ON_VECTOR:
                 vector_stats(k + 1)
             if k < 2:
@@ -297,23 +350,14 @@ def tile_hgnnmodel_pa_kernel(tc, e_nodes, adj, ego_embeddings, ln_gamma, ln_beta
             if k == 2:
                 add_beta_on_tensor(EB_ON_TENSOR[2])
             if k >= 1:
+                finish(k - 1)
+                if k - 1 == FINISH_ON_GPSIMD[0]:
+                    for nt in FINISH_ON_GPSIMD[2:]:
+                        add_beta_on_gpsimd(nt)
                 if k - 3 in FINISH_ON_GPSIMD:
-                    late, c, j = late_stores[FINISH_ON_GPSIMD.index(k - 3)]
-                    nc.sync.dma_start(out=out_v[:, c, j, :], in_=late[:])
-                c, j = divmod(k - 1, 4)
-                o_ = work.tile([P, EMB], F32, name="o_")
-                if k - 1 in FINISH_ON_GPSIMD:
-                    scaled = work.tile([P, EMB], F32, name="scaled")
-                    nc.gpsimd.tensor_scalar(
-                        out=scaled[:], in0=us[k - 1][:], scalar1=rstd[k - 1][:], scalar2=0.0, op0=ALU.mult, op1=ALU.add
-                    )
-                    nc.gpsimd.tensor_tensor(out=o_[:], in0=scaled[:], in1=ebs[k - 1][:], op=ALU.add)
-                    late_stores.append((o_, c, j))
-                else:
-                    nc.vector.scalar_tensor_tensor(
-                        out=o_[:], in0=us[k - 1][:], scalar=rstd[k - 1][:], in1=ebs[k - 1][:], op0=ALU.mult, op1=ALU.add
-                    )
-                    nc.sync.dma_start(out=out_v[:, c, j, :], in_=o_[:])
+                    store(k - 3)
+                if k - 1 not in FINISH_ON_GPSIMD:
+                    store(k - 1)
                     i = EB_ON_TENSOR.index(k - 1) + 2
                     if 3 <= i < len(EB_ON_TENSOR):
                         add_beta_on_tensor(EB_ON_TENSOR[i])

@@ -95,8 +95,8 @@ def tile_hgnnmodel_pa_kernel(tc, e_nodes, adj, ego_embeddings, ln_gamma, ln_beta
 
         def regroup_e(c):
             nc.vector.tensor_copy(
-                out=ge[c][:].rearrange("p (a i) t -> p a t i", i=4),
-                in_=e_raw[c][:].rearrange("p t (a i) -> p a t i", i=4),
+                out=ge[c][:].rearrange("p (a i) t -> p a t i", i=8),
+                in_=e_raw[c][:].rearrange("p t (a i) -> p a t i", i=8),
             )
 
         def quantise_e(c):
@@ -107,8 +107,8 @@ def tile_hgnnmodel_pa_kernel(tc, e_nodes, adj, ego_embeddings, ln_gamma, ln_beta
         def regroup_a(engine_copy, g, c, u):
             cols = slice(256 * u, 256 * (u + 1))
             engine_copy(
-                out=ga[g][c][:, cols, :].rearrange("p (s b r) j -> p b j r s", s=2, r=2),
-                in_=a_raw[g][c][:, :, cols].rearrange("p j (b r s) -> p b j r s", r=2, s=2),
+                out=ga[g][c][:, cols, :].rearrange("p (s b r) j -> p b j r s", s=2, r=4),
+                in_=a_raw[g][c][:, :, cols].rearrange("p j (b r s) -> p b j r s", r=4, s=2),
             )
 
         def quantise_a1(g, c, cols=slice(0, 512)):

@@ -21,6 +21,7 @@ XT_BANKS = ((0, 2), (4, 6))
 MP_BANKS = ((0, 1, 2, 3), (4, 5, 6, 7))
 HP_BANKS = (0, 1, 2, 3, 4, 5, 0, 1)
 EB_BANKS = (6, 7, 2, 6, 7, 2)
+LAST_CUT = 384
 STATS_ON_VECTOR = (0, 2, 5)
 FINISH_ON_GPSIMD = (2, 4)
 EB_ON_TENSOR = (0, 1, 3, 5, 6, 7)
@@ -281,10 +282,14 @@ def tile_hgnnmodel_pa_kernel(tc, e_nodes, adj, ego_embeddings, ln_gamma, ln_beta
                     out=junk[:], in_=hps[nt][:], func=ACT.Identity, scale=-1.0 / EMB, accum_out=negmean[nt][:]
                 )
 
+        partial_stats = {}
+
         def vector_stats(nt):
-            st6 = work.tile([P, 6], F32, name="st6")
-            nc.vector.bn_stats(out=st6[:], in_=hps[nt][:])
-            nc.vector.bn_aggr(out=mv[nt][:], in_=st6[:])
+            partial_stats[nt] = work.tile([P, 6], F32, name="st6")
+            nc.vector.bn_stats(out=partial_stats[nt][:], in_=hps[nt][:])
+
+        def join_stats(nt):
+            nc.vector.bn_aggr(out=mv[nt][:], in_=partial_stats[nt][:])
 
         def squares(nt):
             if on_scalar(nt):
@@ -311,6 +316,9 @@ def tile_hgnnmodel_pa_kernel(tc, e_nodes, adj, ego_embeddings, ln_gamma, ln_beta
 
         finished = {}
 
+        def pieces(nt):
+            return (slice(0, LAST_CUT), slice(LAST_CUT, EMB)) if nt == 7 else (slice(0, EMB),)
+
         def finish(nt):
             o_ = work.tile([P, EMB], F32, name="o_")
             if nt in FINISH_ON_GPSIMD:
@@ -320,14 +328,17 @@ def tile_hgnnmodel_pa_kernel(tc, e_nodes, adj, ego_embeddings, ln_gamma, ln_beta
                 )
                 nc.gpsimd.tensor_tensor(out=o_[:], in0=scaled[:], in1=ebs[nt][:], op=ALU.add)
             else:
-                nc.vector.scalar_tensor_tensor(
-                    out=o_[:], in0=us[nt][:], scalar=rstd[nt][:], in1=ebs[nt][:], op0=ALU.mult, op1=ALU.add
-                )
+                for cols in pieces(nt):
+                    nc.vector.scalar_tensor_tensor(
+                        out=o_[:, cols], in0=us[nt][:, cols], scalar=rstd[nt][:], in1=ebs[nt][:, cols],
+                        op0=ALU.mult, op1=ALU.add,
+                    )
             finished[nt] = o_
 
         def store(nt):
             c, j = divmod(nt, 4)
-            nc.sync.dma_start(out=out_v[:, c, j, :], in_=finished[nt][:])
+            for cols in pieces(nt):
+                nc.sync.dma_start(out=out_v[:, c, j, cols], in_=finished[nt][:, cols])
 
         started = keep.tile([P, 1], U32, name="started")
         nc.gpsimd.tensor_copy(out=started[:], in_=m_codes[1][:, EMB - 1 : EMB])
@@ -335,15 +346,20 @@ def tile_hgnnmodel_pa_kernel(tc, e_nodes, adj, ego_embeddings, ln_gamma, ln_beta
             add_beta_on_gpsimd(nt)
         vector_stats(0)
         vector_stats(2)
+        join_stats(0)
+        join_stats(2)
         for k in range(9):
             minus_mean(k + 1)
+            squares(k)
             if k >= 1:
                 inverse_deviation(k - 1)
-            squares(k)
+            late = k > 1 and k + 1 in STATS_ON_VECTOR
+            if late:
+                vector_stats(k + 1)
             if k < 8:
                 times_gamma(k)
-            if k > 1 and k + 1 in STATS_ON_VECTOR:
-                vector_stats(k + 1)
+            if late:
+                join_stats(k + 1)
             if k < 2:
                 second_matmul(k + 6, 0)
                 second_matmul(k + 6, 1)

@@ -87,9 +87,9 @@ def tile_hgnnmodel_pa_kernel(tc, e_nodes, adj, ego_embeddings, ln_gamma, ln_beta
         ga = grid([P, 512, 4], BF16, "ga")
         a1_codes = grid([P, 512], U32, "a1c")
         a1_scales = grid([P, 512], U8, "a1s")
-        gb = grid([P, 4, P, 2], F32, "gb")
-        a2_codes = grid([P, 512], U32, "a2c")
-        a2_scales = grid([P, 512], U8, "a2s")
+        gb = pair([P, 2, 4, P, 2], F32, "gb")
+        a2_codes = pair([P, 2, 512], U32, "a2c")
+        a2_scales = pair([P, 2, 512], U8, "a2s")
         gm = pair([P, EMB, 4], BF16, "gm")
         m_codes = pair([P, EMB], U32, "mc")
         m_scales = pair([P, EMB], U8, "ms")
@@ -133,15 +133,15 @@ def tile_hgnnmodel_pa_kernel(tc, e_nodes, adj, ego_embeddings, ln_gamma, ln_beta
 
         def copy_words(g, c, jp):
             nc.scalar.copy(
-                out=gb[g][c][:, 2 * jp : 2 * jp + 2, :, :],
+                out=gb[g][:, c, 2 * jp : 2 * jp + 2, :, :],
                 in_=xts[g, c, jp][:].rearrange("q (jj u) n -> q jj n u", u=2),
             )
 
-        def quantise_a2(g, c):
+        def quantise_a2(g):
             nc.vector.quantize_mx(
-                out=a2_codes[g][c][:].bitcast(FP8X4),
-                scales=a2_scales[g][c][:],
-                in_=gb[g][c][:].bitcast(BF16).rearrange("q j n w -> q (j n w)"),
+                out=a2_codes[g][:].rearrange("q c w -> q (c w)").bitcast(FP8X4),
+                scales=a2_scales[g][:].rearrange("q c w -> q (c w)"),
+                in_=gb[g][:].rearrange("q c j n w -> q (c j n w)").bitcast(BF16),
             )
 
         ebs = {}
@@ -178,8 +178,7 @@ def tile_hgnnmodel_pa_kernel(tc, e_nodes, adj, ego_embeddings, ln_gamma, ln_beta
         def copy_m(engine_copy, g, fc):
             engine_copy(out=gm[g][:, P * fc : P * (fc + 1), :], in_=mps[g, fc][:].rearrange("p t f -> p f t"))
 
-        def quantise_m(g, half):
-            cols = slice(256 * half, 256 * (half + 1))
+        def quantise_m(g, cols):
             nc.vector.quantize_mx(
                 out=m_codes[g][:, cols].bitcast(FP8X4),
                 scales=m_scales[g][:, cols],
@@ -194,8 +193,8 @@ def tile_hgnnmodel_pa_kernel(tc, e_nodes, adj, ego_embeddings, ln_gamma, ln_beta
                 hps[nt] = bank(HP_BANKS[nt], [P, EMB], "hp%d" % nt)
             nc.tensor.matmul_mx(
                 out=hps[nt][:],
-                lhsT=a2_codes[g][c][:, P * j : P * (j + 1)].bitcast(FP8X4),
-                lhsT_scale=a2_scales[g][c][:, P * j : P * (j + 1)],
+                lhsT=a2_codes[g][:, c, P * j : P * (j + 1)].bitcast(FP8X4),
+                lhsT_scale=a2_scales[g][:, c, P * j : P * (j + 1)],
                 rhs=m_codes[g][:].bitcast(FP8X4),
                 rhs_scale=m_scales[g][:],
                 start=(g == 0),
@@ -237,17 +236,14 @@ def tile_hgnnmodel_pa_kernel(tc, e_nodes, adj, ego_embeddings, ln_gamma, ln_beta
         first_matmul(0, every, every)
         for fc in every:
             copy_m(scalar_copy, 0, fc)
-        quantise_a2(0, 0)
-        quantise_a2(0, 1)
-        quantise_m(0, 0)
-        quantise_m(0, 1)
+        quantise_a2(0)
+        quantise_m(0, slice(0, EMB))
         first_matmul(1, every, every)
         for fc in every:
             copy_m(scalar_copy, 1, fc)
-        quantise_a2(1, 0)
-        quantise_a2(1, 1)
-        quantise_m(1, 0)
-        quantise_m(1, 1)
+        quantise_a2(1)
+        quantise_m(1, slice(0, 256))
+        quantise_m(1, slice(256, EMB))
         for nt in range(4):
             second_matmul(nt, 0)
         add_beta_on_tensor(EB_ON_TENSOR[0])
@@ -259,7 +255,6 @@ def tile_hgnnmodel_pa_kernel(tc, e_nodes, adj, ego_embeddings, ln_gamma, ln_beta
         add_beta_on_tensor(EB_ON_TENSOR[1])
 
         out_v = out.rearrange("(c p j) f -> p c j f", c=2, j=4)
-        junk = keep.tile([P, EMB], BF16, name="junk")
 
         def on_scalar(nt):
             return 0 <= nt < 8 and nt not in STATS_ON_VECTOR
@@ -278,6 +273,7 @@ def tile_hgnnmodel_pa_kernel(tc, e_nodes, adj, ego_embeddings, ln_gamma, ln_beta
 
         def minus_mean(nt):
             if on_scalar(nt):
+                junk = work.tile([P, EMB], BF16, name="junk")
                 nc.scalar.activation(
                     out=junk[:], in_=hps[nt][:], func=ACT.Identity, scale=-1.0 / EMB, accum_out=negmean[nt][:]
                 )
@@ -293,6 +289,7 @@ def tile_hgnnmodel_pa_kernel(tc, e_nodes, adj, ego_embeddings, ln_gamma, ln_beta
 
         def squares(nt):
             if on_scalar(nt):
+                junk = work.tile([P, EMB], BF16, name="junk")
                 nc.scalar.activation(
                     out=junk[:], in_=hps[nt][:], func=ACT.Square, bias=negmean[nt][:], accum_out=ssd[nt][:]
                 )

from contextlib import ExitStack

import concourse.mybir as mybir
from concourse.masks import make_identity

F32 = mybir.dt.float32
BF16 = mybir.dt.bfloat16
I32 = mybir.dt.int32
U32 = mybir.dt.uint32
U8 = mybir.dt.uint8
FP8X4 = mybir.dt.float8_e4m3fn_x4
ALU = mybir.AluOpType
ACT = mybir.ActivationFunctionType

P = 128
EMB = 512
LN_EPS = 1e-5
FLOPS = 2 * 2 * 1024 * 1024 * 512

XT_BANKS = ((0, 2), (4, 6))
MP_BANKS = ((0, 1, 2, 3), (4, 5, 6, 7))
HP_BANKS = (0, 1, 2, 3, 4, 5, 0, 1)
EB_BANKS = (6, 7, 2, 6, 7, 2)
LAST_CUT = 384
STATS_ON_VECTOR = (0, 2, 5)
FINISH_ON_GPSIMD = (2, 4)
EB_ON_TENSOR = (0, 1, 3, 5, 6, 7)


def tile_hgnnmodel_pa_kernel(tc, e_nodes, adj, ego_embeddings, ln_gamma, ln_beta, out):
    nc = tc.nc
    with ExitStack() as ctx:
        keep = ctx.enter_context(tc.tile_pool(name="keep", bufs=1))
        work = ctx.enter_context(tc.tile_pool(name="work", bufs=8))
        psum = ctx.enter_context(tc.psum_pool(name="psum", bufs=1))
        ctx.enter_context(tc.manual_schedule())

        def bank(b, shape, name):
            return psum.tile(shape, F32, tag="bank%d" % b, name=name)

        def grid(shape, dtype, name):
            return [
                [keep.tile(shape, dtype, name="%s%d%d" % (name, g, c), align_bytes=64) for c in range(2)]
                for g in range(2)
            ]

        def pair(shape, dtype, name):
            return [keep.tile(shape, dtype, name="%s%d" % (name, i), align_bytes=64) for i in range(2)]

        gamma_b = keep.tile([P, EMB], BF16, name="gamma_b")
        beta_b = keep.tile([P, EMB], BF16, name="beta_b")
        e_raw = pair([P, 4, EMB], BF16, "e_raw")
        a_raw = grid([P, 4, 512], BF16, "a_raw")
        ego_raw = pair([P, 4, EMB], BF16, "ego_raw")

        def load_rows(dst, src, c):
            nc.sync.dma_start(out=dst[:], in_=src[512 * c : 512 * (c + 1), :].rearrange("(p j) f -> p j f", j=4))

        def load_a(g, c):
            load_rows(a_raw[g][c], adj[:, 512 * g : 512 * (g + 1)], c)

        load_a(0, 0)
        load_rows(e_raw[0], e_nodes, 0)
        load_a(0, 1)
        load_rows(e_raw[1], e_nodes, 1)
        load_a(1, 0)
        load_a(1, 1)
        load_rows(ego_raw[0], ego_embeddings, 0)
        load_rows(ego_raw[1], ego_embeddings, 1)
        nc.sync.dma_start(out=beta_b[:], in_=ln_beta.partition_broadcast(P))
        nc.sync.dma_start(out=gamma_b[:], in_=ln_gamma.partition_broadcast(P))

        one_col = keep.tile([P, 1], F32, name="one_col")
        nc.vector.memset(one_col[:], 1.0)
        ident = keep.tile([P, P], F32, name="ident")
        make_identity(nc, ident[:])
        ident_bf = keep.tile([P, P], BF16, name="ident_bf")
        make_identity(nc, ident_bf[:])
        warm = keep.tile([P, 1], F32, name="warm")
        nc.scalar.activation(out=warm[:], in_=one_col[:], func=ACT.Abs_reciprocal_sqrt)
        eps_t = keep.tile([P, 1], F32, name="eps_t")
        nc.scalar.mul(out=eps_t[:], in_=one_col[:], mul=LN_EPS)

        ge = pair([P, EMB, 4], BF16, "ge")
        e_codes = pair([P, EMB], U32, "ec")
        e_scales = pair([P, EMB], U8, "es")
        ga = grid([P, 512, 4], BF16, "ga")
        a1_codes = grid([P, 512], U32, "a1c")
        a1_scales = grid([P, 512], U8, "a1s")
        gb = pair([P, 2, 4, P, 2], F32, "gb")
        a2_codes = pair([P, 2, 512], U32, "a2c")
        a2_scales = pair([P, 2, 512], U8, "a2s")
        gm = pair([P, EMB, 4], BF16, "gm")
        m_codes = pair([P, EMB], U32, "mc")
        m_scales = pair([P, EMB], U8, "ms")

        def regroup_e(c):
            nc.vector.tensor_copy(
                out=ge[c][:].rearrange("p (a i) t -> p a t i", i=8),
                in_=e_raw[c][:].rearrange("p t (a i) -> p a t i", i=8),
            )

        def quantise_e(c):
            nc.vector.quantize_mx(
                out=e_codes[c][:].bitcast(FP8X4), scales=e_scales[c][:], in_=ge[c][:].rearrange("p w j -> p (w j)")
            )

        def regroup_a(engine_copy, g, c, u):
            cols = slice(256 * u, 256 * (u + 1))
            engine_copy(
                out=ga[g][c][:, cols, :].rearrange("p (s b r) j -> p b j r s", s=2, r=4),
                in_=a_raw[g][c][:, :, cols].rearrange("p j (b r s) -> p b j r s", r=4, s=2),
            )

        def quantise_a1(g, c, cols=slice(0, 512)):
            nc.vector.quantize_mx(
                out=a1_codes[g][c][:, cols].bitcast(FP8X4),
                scales=a1_scales[g][c][:, cols],
                in_=ga[g][c][:, cols, :].rearrange("p w j -> p (w j)"),
            )

        xts = {}

        def transpose_a(g, c):
            a32 = a_raw[g][c][:].bitcast(F32)
            for jp in range(2):
                xts[g, c, jp] = bank(XT_BANKS[g][c] + jp, [P, 4, P], "xt%d%d%d" % (g, c, jp))
                for jj in range(2):
                    for u in range(2):
                        nc.tensor.transpose(
                            xts[g, c, jp][:, 2 * jj + u, :], a32[:, 2 * jp + jj, P * u : P * (u + 1)], ident[:]
                        )

        def copy_words(g, c, jp):
            nc.scalar.copy(
                out=gb[g][:, c, 2 * jp : 2 * jp + 2, :, :],
                in_=xts[g, c, jp][:].rearrange("q (jj u) n -> q jj n u", u=2),
            )

        def quantise_a2(g):
            nc.vector.quantize_mx(
                out=a2_codes[g][:].rearrange("q c w -> q (c w)").bitcast(FP8X4),
                scales=a2_scales[g][:].rearrange("q c w -> q (c w)"),
                in_=gb[g][:].rearrange("q c j n w -> q (c j n w)").bitcast(BF16),
            )

        ebs = {}

        def add_beta_on_gpsimd(nt):
            c, j = divmod(nt, 4)
            ebs[nt] = keep.tile([P, EMB], F32, name="eb%d" % nt)
            nc.gpsimd.tensor_tensor(out=ebs[nt][:], in0=ego_raw[c][:, j, :], in1=beta_b[:], op=ALU.add)

        def add_beta_on_tensor(nt):
            c, j = divmod(nt, 4)
            ebs[nt] = bank(EB_BANKS[EB_ON_TENSOR.index(nt)], [P, EMB], "ebp%d" % nt)
            nc.tensor.matmul(out=ebs[nt][:], lhsT=ident_bf[:], rhs=ego_raw[c][:, j, :], start=True, stop=False)
            nc.tensor.matmul(out=ebs[nt][:], lhsT=ident_bf[:], rhs=beta_b[:], start=False, stop=True)

        mps = {}

        def first_matmul(g, fcs, ts):
            for fc in fcs:
                if ts[0] == 0:
                    mps[g, fc] = bank(MP_BANKS[g][fc], [P, 4, P], "mp%d%d" % (g, fc))
                for t in ts:
                    for c in range(2):
                        nc.tensor.matmul_mx(
                            out=mps[g, fc][:, t, :],
                            lhsT=a1_codes[g][c][:, P * t : P * (t + 1)].bitcast(FP8X4),
                            lhsT_scale=a1_scales[g][c][:, P * t : P * (t + 1)],
                            rhs=e_codes[c][:, P * fc : P * (fc + 1)].bitcast(FP8X4),
                            rhs_scale=e_scales[c][:, P * fc : P * (fc + 1)],
                            start=(c == 0),
                            stop=(c == 1),
                        )

        def copy_m(engine_copy, g, fc):
            engine_copy(out=gm[g][:, P * fc : P * (fc + 1), :], in_=mps[g, fc][:].rearrange("p t f -> p f t"))

        def quantise_m(g, cols):
            nc.vector.quantize_mx(
                out=m_codes[g][:, cols].bitcast(FP8X4),
                scales=m_scales[g][:, cols],
                in_=gm[g][:, cols, :].rearrange("p w j -> p (w j)"),
            )

        hps = {}

        def second_matmul(nt, g):
            c, j = divmod(nt, 4)
            if g == 0:
                hps[nt] = bank(HP_BANKS[nt], [P, EMB], "hp%d" % nt)
            nc.tensor.matmul_mx(
                out=hps[nt][:],
                lhsT=a2_codes[g][:, c, P * j : P * (j + 1)].bitcast(FP8X4),
                lhsT_scale=a2_scales[g][:, c, P * j : P * (j + 1)],
                rhs=m_codes[g][:].bitcast(FP8X4),
                rhs_scale=m_scales[g][:],
                start=(g == 0),
                stop=(g == 1),
            )

        vector_copy = nc.vector.tensor_copy
        scalar_copy = nc.scalar.copy

        every = range(4)
        regroup_a(vector_copy, 0, 0, 0)
        regroup_a(vector_copy, 0, 0, 1)
        transpose_a(0, 0)
        copy_words(0, 0, 0)
        copy_words(0, 0, 1)
        regroup_e(0)
        quantise_a1(0, 0)
        regroup_a(vector_copy, 0, 1, 0)
        regroup_a(scalar_copy, 0, 1, 1)
        transpose_a(0, 1)
        copy_words(0, 1, 0)
        copy_words(0, 1, 1)
        quantise_e(0)
        regroup_e(1)
        quantise_a1(0, 1)
        quantise_e(1)
        regroup_a(vector_copy, 1, 0, 0)
        regroup_a(scalar_copy, 1, 0, 1)
        transpose_a(1, 0)
        copy_words(1, 0, 0)
        copy_words(1, 0, 1)
        regroup_a(vector_copy, 1, 1, 0)
        regroup_a(vector_copy, 1, 1, 1)
        transpose_a(1, 1)
        copy_words(1, 1, 0)
        copy_words(1, 1, 1)
        quantise_a1(1, 0)
        quantise_a1(1, 1)
        first_matmul(0, every, every)
        for fc in every:
            copy_m(scalar_copy, 0, fc)
        quantise_a2(0)
        quantise_m(0, slice(0, EMB))
        first_matmul(1, every, every)
        for fc in every:
            copy_m(scalar_copy, 1, fc)
        quantise_a2(1)
        quantise_m(1, slice(0, 256))
        quantise_m(1, slice(256, EMB))
        for nt in range(4):
            second_matmul(nt, 0)
        add_beta_on_tensor(EB_ON_TENSOR[0])
        for nt in range(4):
            second_matmul(nt, 1)
        for nt in range(4, 6):
            second_matmul(nt, 0)
            second_matmul(nt, 1)
        add_beta_on_tensor(EB_ON_TENSOR[1])

        out_v = out.rearrange("(c p j) f -> p c j f", c=2, j=4)

        def on_scalar(nt):
            return 0 <= nt < 8 and nt not in STATS_ON_VECTOR

        negmean = {}
        ssd = {}
        mv = {}
        for nt in range(8):
            if on_scalar(nt):
                negmean[nt] = keep.tile([P, 1], F32, name="negmean%d" % nt)
                ssd[nt] = keep.tile([P, 1], F32, name="ssd%d" % nt)
            else:
                mv[nt] = keep.tile([P, 2], F32, name="mv%d" % nt)
        rstd = [keep.tile([P, 1], F32, name="rstd%d" % nt) for nt in range(8)]
        us = [keep.tile([P, EMB], F32, name="u%d" % nt) for nt in range(8)]

        def minus_mean(nt):
            if on_scalar(nt):
                junk = work.tile([P, EMB], BF16, name="junk")
                nc.scalar.activation(
                    out=junk[:], in_=hps[nt][:], func=ACT.Identity, scale=-1.0 / EMB, accum_out=negmean[nt][:]
                )

        partial_stats = {}

        def vector_stats(nt):
            partial_stats[nt] = work.tile([P, 6], F32, name="st6")
            nc.vector.bn_stats(out=partial_stats[nt][:], in_=hps[nt][:])

        def join_stats(nt):
            nc.vector.bn_aggr(out=mv[nt][:], in_=partial_stats[nt][:])

        def squares(nt):
            if on_scalar(nt):
                junk = work.tile([P, EMB], BF16, name="junk")
                nc.scalar.activation(
                    out=junk[:], in_=hps[nt][:], func=ACT.Square, bias=negmean[nt][:], accum_out=ssd[nt][:]
                )

        def inverse_deviation(nt):
            variance, scale = (ssd[nt][:], 1.0 / EMB) if on_scalar(nt) else (mv[nt][:, 1:2], 1.0)
            nc.scalar.activation(
                out=rstd[nt][:], in_=variance, func=ACT.Abs_reciprocal_sqrt, bias=eps_t[:], scale=scale
            )

        def times_gamma(nt):
            if on_scalar(nt):
                nc.vector.scalar_tensor_tensor(
                    out=us[nt][:], in0=hps[nt][:], scalar=negmean[nt][:], in1=gamma_b[:], op0=ALU.add, op1=ALU.mult
                )
            else:
                nc.vector.scalar_tensor_tensor(
                    out=us[nt][:], in0=hps[nt][:], scalar=mv[nt][:, 0:1], in1=gamma_b[:],
                    op0=ALU.subtract, op1=ALU.mult,
                )

        finished = {}

        def pieces(nt):
            return (slice(0, LAST_CUT), slice(LAST_CUT, EMB)) if nt == 7 else (slice(0, EMB),)

        def finish(nt):
            o_ = work.tile([P, EMB], F32, name="o_")
            if nt in FINISH_ON_GPSIMD:
                scaled = work.tile([P, EMB], F32, name="scaled")
                nc.gpsimd.tensor_scalar(
                    out=scaled[:], in0=us[nt][:], scalar1=rstd[nt][:], scalar2=0.0, op0=ALU.mult, op1=ALU.add
                )
                nc.gpsimd.tensor_tensor(out=o_[:], in0=scaled[:], in1=ebs[nt][:], op=ALU.add)
            else:
                for cols in pieces(nt):
                    nc.vector.scalar_tensor_tensor(
                        out=o_[:, cols], in0=us[nt][:, cols], scalar=rstd[nt][:], in1=ebs[nt][:, cols],
                        op0=ALU.mult, op1=ALU.add,
                    )
            finished[nt] = o_

        def store(nt):
            c, j = divmod(nt, 4)
            for cols in pieces(nt):
                nc.sync.dma_start(out=out_v[:, c, j, cols], in_=finished[nt][:, cols])

        started = keep.tile([P, 1], U32, name="started")
        nc.gpsimd.tensor_copy(out=started[:], in_=m_codes[1][:, EMB - 1 : EMB])
        for nt in FINISH_ON_GPSIMD[:2]:
            add_beta_on_gpsimd(nt)
        vector_stats(0)
        vector_stats(2)
        join_stats(0)
        join_stats(2)
        for k in range(9):
            minus_mean(k + 1)
            squares(k)
            if k >= 1:
                inverse_deviation(k - 1)
            late = k > 1 and k + 1 in STATS_ON_VECTOR
            if late:
                vector_stats(k + 1)
            if k < 8:
                times_gamma(k)
            if late:
                join_stats(k + 1)
            if k < 2:
                second_matmul(k + 6, 0)
                second_matmul(k + 6, 1)
            if k == 2:
                add_beta_on_tensor(EB_ON_TENSOR[2])
            if k >= 1:
                finish(k - 1)
                if k - 1 == FINISH_ON_GPSIMD[0]:
                    for nt in FINISH_ON_GPSIMD[2:]:
                        add_beta_on_gpsimd(nt)
                if k - 3 in FINISH_ON_GPSIMD:
                    store(k - 3)
                if k - 1 not in FINISH_ON_GPSIMD:
                    store(k - 1)
                    i = EB_ON_TENSOR.index(k - 1) + 2
                    if 3 <= i < len(EB_ON_TENSOR):
                        add_beta_on_tensor(EB_ON_TENSOR[i])
